import numpy as np
import ml_dtypes


def mxq(x, axis, fmt="e4m3"):
    dtype, down = {"e4m3": (ml_dtypes.float8_e4m3fn, 7), "e5m2": (ml_dtypes.float8_e5m2, 14)}[fmt]
    v = np.moveaxis(np.asarray(x, np.float32).astype(ml_dtypes.bfloat16).astype(np.float64), axis, -1)
    blocks = v.reshape(v.shape[:-1] + (-1, 32))
    amax = np.abs(blocks).max(-1, keepdims=True)
    byte = np.maximum(np.where(amax > 0, np.frexp(amax)[1] - 1 + 127, 0) - down, 1)
    scale = np.exp2(byte - 127.0)
    codes = (blocks / scale).astype(np.float32).astype(dtype).astype(np.float64)
    return np.moveaxis((codes * scale).reshape(v.shape), -1, axis)


WIDE = False


def mx_kscale(k):
    if not WIDE:
        return np.ones(k)
    levels = np.array([10, -10, 5, -5, 0])
    a = np.random.permutation(np.resize(levels, k // 512 * 4)).reshape(k // 512, 4)
    idx = np.arange(k)
    return np.exp2(a[idx // 512, idx % 128 // 32])


BF16 = ml_dtypes.bfloat16


def bf(x):
    return np.asarray(x, np.float32).astype(BF16)


def f64(x):
    return np.asarray(x).astype(np.float64)


N, IN_DIM, HID, OUT_DIM = 1024, 1024, 512, 256


def setup_inputs():
    t = mx_kscale(HID)
    h1 = np.random.standard_normal((1, HID)) * 0.55 + np.random.standard_normal((N, HID)) * 0.55
    return {"A": bf(np.random.uniform(0.0, 1.0, (N, N)) * 0.5 / np.sqrt(N)),
            "h1": bf(h1 * t),
            "eps1": bf(np.random.uniform(0.2, 0.4, (1,))),
            "W1_1": bf(np.random.standard_normal((HID, HID)) * 0.4 / np.sqrt(HID) / t[:, None]),
            "b1_1": bf(np.random.standard_normal(HID) * 0.2)}


def reference(A, h1, eps1, W1_1, b1_1):
    x = f64(h1)
    z = (mxq(f64(A), 1, "e4m3") @ mxq(x, 0, "e4m3")) + (1.0 + f64(eps1)) * x
    return np.maximum((mxq(z, 1, "e4m3") @ mxq(f64(W1_1), 0, "e4m3")) + f64(b1_1), 0.0)

@@ -1,0 +1,216 @@
+from contextlib import ExitStack
+
+import concourse.mybir as mybir
+from concourse.masks import make_identity
+
+F32 = mybir.dt.float32
+BF16 = mybir.dt.bfloat16
+U32 = mybir.dt.uint32
+U8 = mybir.dt.uint8
+FP8X4 = mybir.dt.float8_e4m3fn_x4
+ALU = mybir.AluOpType
+ACT = mybir.ActivationFunctionType
+
+P = 128
+PACK = 4
+K_PASS = P * PACK
+NODES = 1024
+HID = 512
+NODE_PASSES = NODES // K_PASS
+CHUNKS = NODES // P
+PAIRS = CHUNKS // 2
+ROW_WORDS = NODES // 2
+HID_WORDS = HID // 2
+
+FLOPS = 2 * NODES * NODES * HID + 2 * NODES * HID * HID
+
+
+def tile_gin_pb_kernel(tc, A, h1, eps1, W1_1, b1_1, out):
+    nc = tc.nc
+    with ExitStack() as ctx:
+        keep = ctx.enter_context(tc.tile_pool(name="keep", bufs=1))
+        psum_t = ctx.enter_context(tc.psum_pool(name="psum_t", bufs=4))
+        psum_z = ctx.enter_context(tc.psum_pool(name="psum_z", bufs=2))
+        psum_o = ctx.enter_context(tc.psum_pool(name="psum_o", bufs=2))
+
+        h1_sb = keep.tile([P, CHUNKS * HID], BF16)
+        a_sb = keep.tile([P, CHUNKS * NODES], BF16)
+        w_sb = keep.tile([P, PACK * HID], BF16)
+
+        h_grouped = keep.tile([P, NODE_PASSES * HID * PACK], BF16, align_bytes=64)
+        h_codes = keep.tile([P, NODE_PASSES * HID], U32, align_bytes=64)
+        h_scales = keep.tile([P, NODE_PASSES * HID], U8, align_bytes=64)
+        w_grouped = keep.tile([P, HID * PACK], BF16, align_bytes=64)
+        w_codes = keep.tile([P, HID], U32, align_bytes=64)
+        w_scales = keep.tile([P, HID], U8, align_bytes=64)
+        a_grouped = keep.tile([P, CHUNKS * NODE_PASSES * P * PACK], BF16, align_bytes=64)
+        a_codes = keep.tile([P, CHUNKS * NODE_PASSES * P], U32, align_bytes=64)
+        a_scales = keep.tile([P, CHUNKS * NODE_PASSES * P], U8, align_bytes=64)
+        z_grouped = keep.tile([P, CHUNKS * P * PACK], BF16, align_bytes=64)
+        z_codes = keep.tile([P, CHUNKS * P], U32, align_bytes=64)
+        z_scales = keep.tile([P, CHUNKS * P], U8, align_bytes=64)
+
+        hT_sb = keep.tile([P, CHUNKS * P * PACK], BF16)
+        o_sum = keep.tile([P, CHUNKS * HID], F32)
+        o_sb = keep.tile([P, CHUNKS * HID], F32)
+
+        ident = keep.tile([P, P], F32)
+        ones = keep.tile([P, P], BF16)
+        b_rows = keep.tile([P, HID], BF16)
+        b_all = keep.tile([P, HID], F32)
+        eps_col = keep.tile([P, 1], BF16)
+        self_w = keep.tile([P, 1], F32)
+
+        for g in range(NODE_PASSES):
+            nc.sync.dma_start(
+                out=h1_sb[:, g * PACK * HID : (g + 1) * PACK * HID].rearrange(
+                    "p (u r) -> p u r", u=2
+                ),
+                in_=h1[g * K_PASS : (g + 1) * K_PASS, :].rearrange(
+                    "(u p e) f -> p u (e f)", u=2, e=2
+                ),
+            )
+        nc.sync.dma_start(
+            out=w_sb[:].rearrange("p (v r) -> p v r", v=2),
+            in_=W1_1.rearrange("(v p e) o -> p v (e o)", v=2, e=2),
+        )
+        for h in range(PAIRS):
+            nc.sync.dma_start(
+                out=a_sb[:, h * 2 * NODES : (h + 1) * 2 * NODES],
+                in_=A[h * 2 * P : (h + 1) * 2 * P, :].rearrange("(p e) k -> p (e k)", e=2),
+            )
+
+        make_identity(nc, ident[:])
+        nc.vector.memset(ones[:], 1.0)
+        nc.vector.memset(b_rows[:], 0.0)
+        nc.scalar.dma_start(out=b_rows[0:1, :], in_=b1_1.rearrange("(r o) -> r o", r=1))
+        with nc.allow_non_contiguous_dma(reason="one bfloat16 scalar to every partition"):
+            nc.scalar.dma_start(out=eps_col[:], in_=eps1.partition_broadcast(P))
+        nc.vector.tensor_scalar(
+            out=self_w[:], in0=eps_col[:], scalar1=1.0, scalar2=None, op0=ALU.add
+        )
+        b_bank = psum_t.tile([P, HID], F32, tag="t")
+        nc.tensor.matmul(out=b_bank[:], lhsT=ones[:], rhs=b_rows[:], start=True, stop=True)
+        nc.scalar.copy(out=b_all[:], in_=b_bank[:])
+
+        h1_rows = h1_sb[:].rearrange(
+            "p (g t v q e) -> p g v q t e", g=NODE_PASSES, t=PACK, v=2, e=2
+        )
+        h_slots = h_grouped[:].rearrange(
+            "p (g v e q t) -> p g v q t e", g=NODE_PASSES, v=2, e=2, t=PACK
+        )
+        for g in range(NODE_PASSES):
+            for v in range(2):
+                nc.vector.tensor_copy(out=h_slots[:, g, v], in_=h1_rows[:, g, v])
+        for g in range(NODE_PASSES):
+            nc.vector.quantize_mx(
+                out=h_codes[:, g * HID : (g + 1) * HID].bitcast(FP8X4),
+                scales=h_scales[:, g * HID : (g + 1) * HID],
+                in_=h_grouped[:, g * HID * PACK : (g + 1) * HID * PACK],
+            )
+
+        h1_words = h1_sb[:].bitcast(F32)
+        hT_words = hT_sb[:].bitcast(F32).rearrange("p (c n v) -> p c n v", c=CHUNKS, v=2)
+        for h in range(PAIRS):
+            hT_bank = psum_t.tile([P, 2, 2, P], F32, tag="t")
+            for i in range(2):
+                for v in range(2):
+                    first = (2 * h + i) * HID_WORDS + v * P
+                    nc.tensor.transpose(
+                        hT_bank[:, i, v, :], h1_words[:, first : first + P], ident[:]
+                    )
+            nc.scalar.copy(
+                out=hT_words[:, 2 * h : 2 * h + 2],
+                in_=hT_bank[:].rearrange("p i v n -> p i n v"),
+            )
+
+        nc.scalar.copy(
+            out=w_grouped[:].rearrange("p (c i t) -> p c t i", i=4, t=PACK),
+            in_=w_sb[:].rearrange("p (t c i) -> p c t i", t=PACK, i=4),
+        )
+        nc.vector.quantize_mx(
+            out=w_codes[:].bitcast(FP8X4), scales=w_scales[:], in_=w_grouped[:]
+        )
+
+        a_words = a_sb[:].bitcast(F32)
+        a_slots = a_grouped[:].bitcast(F32).rearrange(
+            "p (c g n u) -> p c g n u", c=CHUNKS, g=NODE_PASSES, u=2
+        )
+        out_rows = out.rearrange("(h p e) o -> p h (e o)", h=PAIRS, e=2)
+
+        def transpose_and_quantise_a(h):
+            for c in (2 * h, 2 * h + 1):
+                a_bank = psum_t.tile([P, NODE_PASSES, 2, P], F32, tag="t")
+                for g in range(NODE_PASSES):
+                    for u in range(2):
+                        first = c * ROW_WORDS + (2 * g + u) * P
+                        nc.tensor.transpose(
+                            a_bank[:, g, u, :], a_words[:, first : first + P], ident[:]
+                        )
+                nc.scalar.copy(
+                    out=a_slots[:, c], in_=a_bank[:].rearrange("p g u n -> p g n u")
+                )
+            width = 2 * NODE_PASSES * P
+            nc.vector.quantize_mx(
+                out=a_codes[:, h * width : (h + 1) * width].bitcast(FP8X4),
+                scales=a_scales[:, h * width : (h + 1) * width],
+                in_=a_grouped[:, h * width * PACK : (h + 1) * width * PACK],
+            )
+
+        def aggregate_and_quantise_z(h):
+            for c in (2 * h, 2 * h + 1):
+                z_bank = psum_z.tile([P, PACK, P], F32)
+                for t in range(PACK):
+                    for g in range(NODE_PASSES):
+                        feats = slice(g * HID + t * P, g * HID + (t + 1) * P)
+                        nodes = slice((c * NODE_PASSES + g) * P, (c * NODE_PASSES + g + 1) * P)
+                        nc.tensor.matmul_mx(
+                            out=z_bank[:, t, :],
+                            lhsT=h_codes[:, feats].bitcast(FP8X4),
+                            lhsT_scale=h_scales[:, feats],
+                            rhs=a_codes[:, nodes].bitcast(FP8X4),
+                            rhs_scale=a_scales[:, nodes],
+                            start=(g == 0),
+                            stop=(g == NODE_PASSES - 1),
+                        )
+                cols = slice(c * P * PACK, (c + 1) * P * PACK)
+                nc.vector.scalar_tensor_tensor(
+                    out=z_grouped[:, cols].rearrange("p (n t) -> p n t", t=PACK),
+                    in0=hT_sb[:, cols].rearrange("p (n t) -> p n t", t=PACK),
+                    scalar=self_w[:, 0:1],
+                    in1=z_bank[:].rearrange("p t n -> p n t"),
+                    op0=ALU.mult,
+                    op1=ALU.add,
+                )
+            nc.vector.quantize_mx(
+                out=z_codes[:, h * 2 * P : (h + 1) * 2 * P].bitcast(FP8X4),
+                scales=z_scales[:, h * 2 * P : (h + 1) * 2 * P],
+                in_=z_grouped[:, h * 2 * P * PACK : (h + 1) * 2 * P * PACK],
+            )
+
+        def linear_relu_store(h):
+            for c in (2 * h, 2 * h + 1):
+                o_bank = psum_o.tile([P, HID], F32)
+                nc.tensor.matmul_mx(
+                    out=o_bank[:],
+                    lhsT=z_codes[:, c * P : (c + 1) * P].bitcast(FP8X4),
+                    lhsT_scale=z_scales[:, c * P : (c + 1) * P],
+                    rhs=w_codes[:].bitcast(FP8X4),
+                    rhs_scale=w_scales[:],
+                    start=True,
+                    stop=True,
+                )
+                nc.vector.tensor_tensor(
+                    out=o_sum[:, c * HID : (c + 1) * HID], in0=o_bank[:], in1=b_all[:], op=ALU.add
+                )
+            both = slice(h * 2 * HID, (h + 1) * 2 * HID)
+            nc.scalar.activation(out=o_sb[:, both], in_=o_sum[:, both], func=ACT.Relu)
+            nc.sync.dma_start(out=out_rows[:, h, :], in_=o_sb[:, both])
+
+        for step in range(PAIRS + 2):
+            if step < PAIRS:
+                transpose_and_quantise_a(step)
+            if 1 <= step <= PAIRS:
+                aggregate_and_quantise_z(step - 1)
+            if step >= 2:
+                linear_relu_store(step - 2)

@@ -25,6 +25,10 @@ HID_WORDS = HID // 2
 FLOPS = 2 * NODES * NODES * HID + 2 * NODES * HID * HID
 
 
+LAG_LINEAR = 2
+LAG_BIAS = 3
+
+
 def tile_gin_pb_kernel(tc, A, h1, eps1, W1_1, b1_1, out):
     nc = tc.nc
     with ExitStack() as ctx:
@@ -32,6 +36,7 @@ def tile_gin_pb_kernel(tc, A, h1, eps1, W1_1, b1_1, out):
         psum_t = ctx.enter_context(tc.psum_pool(name="psum_t", bufs=4))
         psum_z = ctx.enter_context(tc.psum_pool(name="psum_z", bufs=2))
         psum_o = ctx.enter_context(tc.psum_pool(name="psum_o", bufs=2))
+        ctx.enter_context(tc.manual_schedule())
 
         h1_sb = keep.tile([P, CHUNKS * HID], BF16)
         a_sb = keep.tile([P, CHUNKS * NODES], BF16)
@@ -61,37 +66,39 @@ def tile_gin_pb_kernel(tc, A, h1, eps1, W1_1, b1_1, out):
         eps_col = keep.tile([P, 1], BF16)
         self_w = keep.tile([P, 1], F32)
 
-        for g in range(NODE_PASSES):
+        nc.vector.memset(b_rows[:], 0.0)
+        nc.sync.dma_start(out=b_rows[0:1, :], in_=b1_1.rearrange("(r o) -> r o", r=1))
+        with nc.allow_non_contiguous_dma(reason="one bfloat16 scalar to every partition"):
+            nc.sync.dma_start(out=eps_col[:], in_=eps1.partition_broadcast(P))
+
+        def load_h1(h):
             nc.sync.dma_start(
-                out=h1_sb[:, g * PACK * HID : (g + 1) * PACK * HID].rearrange(
-                    "p (u r) -> p u r", u=2
-                ),
-                in_=h1[g * K_PASS : (g + 1) * K_PASS, :].rearrange(
-                    "(u p e) f -> p u (e f)", u=2, e=2
-                ),
+                out=h1_sb[:, h * 2 * HID : (h + 1) * 2 * HID],
+                in_=h1[h * 2 * P : (h + 1) * 2 * P, :].rearrange("(p e) f -> p (e f)", e=2),
             )
-        nc.sync.dma_start(
-            out=w_sb[:].rearrange("p (v r) -> p v r", v=2),
-            in_=W1_1.rearrange("(v p e) o -> p v (e o)", v=2, e=2),
-        )
-        for h in range(PAIRS):
+
+        def load_a(h):
             nc.sync.dma_start(
                 out=a_sb[:, h * 2 * NODES : (h + 1) * 2 * NODES],
                 in_=A[h * 2 * P : (h + 1) * 2 * P, :].rearrange("(p e) k -> p (e k)", e=2),
             )
 
+        for h in range(PAIRS):
+            load_h1(h)
+        load_a(0)
+        load_a(1)
+        nc.sync.dma_start(
+            out=w_sb[:].rearrange("p (v r) -> p v r", v=2),
+            in_=W1_1.rearrange("(v p e) o -> p v (e o)", v=2, e=2),
+        )
+        load_a(2)
+        load_a(3)
+
         make_identity(nc, ident[:])
         nc.vector.memset(ones[:], 1.0)
-        nc.vector.memset(b_rows[:], 0.0)
-        nc.scalar.dma_start(out=b_rows[0:1, :], in_=b1_1.rearrange("(r o) -> r o", r=1))
-        with nc.allow_non_contiguous_dma(reason="one bfloat16 scalar to every partition"):
-            nc.scalar.dma_start(out=eps_col[:], in_=eps1.partition_broadcast(P))
         nc.vector.tensor_scalar(
             out=self_w[:], in0=eps_col[:], scalar1=1.0, scalar2=None, op0=ALU.add
         )
-        b_bank = psum_t.tile([P, HID], F32, tag="t")
-        nc.tensor.matmul(out=b_bank[:], lhsT=ones[:], rhs=b_rows[:], start=True, stop=True)
-        nc.scalar.copy(out=b_all[:], in_=b_bank[:])
 
         h1_rows = h1_sb[:].rearrange(
             "p (g t v q e) -> p g v q t e", g=NODE_PASSES, t=PACK, v=2, e=2
@@ -99,19 +106,15 @@ def tile_gin_pb_kernel(tc, A, h1, eps1, W1_1, b1_1, out):
         h_slots = h_grouped[:].rearrange(
             "p (g v e q t) -> p g v q t e", g=NODE_PASSES, v=2, e=2, t=PACK
         )
-        for g in range(NODE_PASSES):
-            for v in range(2):
-                nc.vector.tensor_copy(out=h_slots[:, g, v], in_=h1_rows[:, g, v])
-        for g in range(NODE_PASSES):
-            nc.vector.quantize_mx(
-                out=h_codes[:, g * HID : (g + 1) * HID].bitcast(FP8X4),
-                scales=h_scales[:, g * HID : (g + 1) * HID],
-                in_=h_grouped[:, g * HID * PACK : (g + 1) * HID * PACK],
-            )
-
         h1_words = h1_sb[:].bitcast(F32)
         hT_words = hT_sb[:].bitcast(F32).rearrange("p (c n v) -> p c n v", c=CHUNKS, v=2)
-        for h in range(PAIRS):
+        a_words = a_sb[:].bitcast(F32)
+        a_slots = a_grouped[:].bitcast(F32).rearrange(
+            "p (c g n u) -> p c g n u", c=CHUNKS, g=NODE_PASSES, u=2
+        )
+        out_rows = out.rearrange("(h p e) o -> p h e o", h=PAIRS, e=2)
+
+        def transpose_h1(h):
             hT_bank = psum_t.tile([P, 2, 2, P], F32, tag="t")
             for i in range(2):
                 for v in range(2):
@@ -124,93 +127,127 @@ def tile_gin_pb_kernel(tc, A, h1, eps1, W1_1, b1_1, out):
                 in_=hT_bank[:].rearrange("p i v n -> p i n v"),
             )
 
+        def regroup_h1(g, v):
+            nc.vector.tensor_copy(out=h_slots[:, g, v], in_=h1_rows[:, g, v])
+
+        def quantise_h1(g):
+            nc.vector.quantize_mx(
+                out=h_codes[:, g * HID : (g + 1) * HID].bitcast(FP8X4),
+                scales=h_scales[:, g * HID : (g + 1) * HID],
+                in_=h_grouped[:, g * HID * PACK : (g + 1) * HID * PACK],
+            )
+
+        def transpose_a(c):
+            a_bank = psum_t.tile([P, NODE_PASSES, 2, P], F32, tag="t")
+            for g in range(NODE_PASSES):
+                for u in range(2):
+                    first = c * ROW_WORDS + (2 * g + u) * P
+                    nc.tensor.transpose(
+                        a_bank[:, g, u, :], a_words[:, first : first + P], ident[:]
+                    )
+            nc.scalar.copy(out=a_slots[:, c], in_=a_bank[:].rearrange("p g u n -> p g n u"))
+
+        def quantise_a(c):
+            width = NODE_PASSES * P
+            nc.vector.quantize_mx(
+                out=a_codes[:, c * width : (c + 1) * width].bitcast(FP8X4),
+                scales=a_scales[:, c * width : (c + 1) * width],
+                in_=a_grouped[:, c * width * PACK : (c + 1) * width * PACK],
+            )
+
+        z_banks = {}
+        o_banks = {}
+
+        def aggregate(c):
+            z_banks[c] = psum_z.tile([P, PACK, P], F32, name="z_bank")
+            for t in range(PACK):
+                for g in range(NODE_PASSES):
+                    feats = slice(g * HID + t * P, g * HID + (t + 1) * P)
+                    nodes = slice((c * NODE_PASSES + g) * P, (c * NODE_PASSES + g + 1) * P)
+                    nc.tensor.matmul_mx(
+                        out=z_banks[c][:, t, :],
+                        lhsT=h_codes[:, feats].bitcast(FP8X4),
+                        lhsT_scale=h_scales[:, feats],
+                        rhs=a_codes[:, nodes].bitcast(FP8X4),
+                        rhs_scale=a_scales[:, nodes],
+                        start=(g == 0),
+                        stop=(g == NODE_PASSES - 1),
+                    )
+
+        def add_self_term(c):
+            cols = slice(c * P * PACK, (c + 1) * P * PACK)
+            nc.vector.scalar_tensor_tensor(
+                out=z_grouped[:, cols].rearrange("p (n t) -> p n t", t=PACK),
+                in0=hT_sb[:, cols].rearrange("p (n t) -> p n t", t=PACK),
+                scalar=self_w[:, 0:1],
+                in1=z_banks[c][:].rearrange("p t n -> p n t"),
+                op0=ALU.mult,
+                op1=ALU.add,
+            )
+
+        def quantise_z(c):
+            nc.vector.quantize_mx(
+                out=z_codes[:, c * P : (c + 1) * P].bitcast(FP8X4),
+                scales=z_scales[:, c * P : (c + 1) * P],
+                in_=z_grouped[:, c * P * PACK : (c + 1) * P * PACK],
+            )
+
+        def linear(c):
+            o_banks[c] = psum_o.tile([P, HID], F32, name="o_bank")
+            nc.tensor.matmul_mx(
+                out=o_banks[c][:],
+                lhsT=z_codes[:, c * P : (c + 1) * P].bitcast(FP8X4),
+                lhsT_scale=z_scales[:, c * P : (c + 1) * P],
+                rhs=w_codes[:].bitcast(FP8X4),
+                rhs_scale=w_scales[:],
+                start=True,
+                stop=True,
+            )
+
+        def bias_relu_store(c):
+            cols = slice(c * HID, (c + 1) * HID)
+            nc.vector.tensor_tensor(out=o_sum[:, cols], in0=o_banks[c][:], in1=b_all[:], op=ALU.add)
+            nc.scalar.activation(out=o_sb[:, cols], in_=o_sum[:, cols], func=ACT.Relu)
+            nc.sync.dma_start(out=out_rows[:, c // 2, c % 2, :], in_=o_sb[:, cols])
+
+        for h in range(PAIRS):
+            transpose_h1(h)
+        regroup_h1(0, 0)
+        regroup_h1(0, 1)
+        regroup_h1(1, 0)
+        quantise_h1(0)
+        regroup_h1(1, 1)
+        for c in range(4):
+            transpose_a(c)
+        quantise_a(0)
+        quantise_h1(1)
+        quantise_a(1)
+        aggregate(0)
+        b_bank = psum_t.tile([P, HID], F32, tag="t")
+        nc.tensor.matmul(out=b_bank[:], lhsT=ones[:], rhs=b_rows[:], start=True, stop=True)
+        nc.scalar.copy(out=b_all[:], in_=b_bank[:])
         nc.scalar.copy(
             out=w_grouped[:].rearrange("p (c i t) -> p c t i", i=4, t=PACK),
             in_=w_sb[:].rearrange("p (t c i) -> p c t i", t=PACK, i=4),
         )
-        nc.vector.quantize_mx(
-            out=w_codes[:].bitcast(FP8X4), scales=w_scales[:], in_=w_grouped[:]
-        )
 
-        a_words = a_sb[:].bitcast(F32)
-        a_slots = a_grouped[:].bitcast(F32).rearrange(
-            "p (c g n u) -> p c g n u", c=CHUNKS, g=NODE_PASSES, u=2
-        )
-        out_rows = out.rearrange("(h p e) o -> p h (e o)", h=PAIRS, e=2)
-
-        def transpose_and_quantise_a(h):
-            for c in (2 * h, 2 * h + 1):
-                a_bank = psum_t.tile([P, NODE_PASSES, 2, P], F32, tag="t")
-                for g in range(NODE_PASSES):
-                    for u in range(2):
-                        first = c * ROW_WORDS + (2 * g + u) * P
-                        nc.tensor.transpose(
-                            a_bank[:, g, u, :], a_words[:, first : first + P], ident[:]
-                        )
-                nc.scalar.copy(
-                    out=a_slots[:, c], in_=a_bank[:].rearrange("p g u n -> p g n u")
+        for step in range(CHUNKS + LAG_BIAS):
+            if step + 1 < CHUNKS:
+                aggregate(step + 1)
+            if step == LAG_LINEAR:
+                nc.vector.quantize_mx(
+                    out=w_codes[:].bitcast(FP8X4), scales=w_scales[:], in_=w_grouped[:]
                 )
-            width = 2 * NODE_PASSES * P
-            nc.vector.quantize_mx(
-                out=a_codes[:, h * width : (h + 1) * width].bitcast(FP8X4),
-                scales=a_scales[:, h * width : (h + 1) * width],
-                in_=a_grouped[:, h * width * PACK : (h + 1) * width * PACK],
-            )
-
-        def aggregate_and_quantise_z(h):
-            for c in (2 * h, 2 * h + 1):
-                z_bank = psum_z.tile([P, PACK, P], F32)
-                for t in range(PACK):
-                    for g in range(NODE_PASSES):
-                        feats = slice(g * HID + t * P, g * HID + (t + 1) * P)
-                        nodes = slice((c * NODE_PASSES + g) * P, (c * NODE_PASSES + g + 1) * P)
-                        nc.tensor.matmul_mx(
-                            out=z_bank[:, t, :],
-                            lhsT=h_codes[:, feats].bitcast(FP8X4),
-                            lhsT_scale=h_scales[:, feats],
-                            rhs=a_codes[:, nodes].bitcast(FP8X4),
-                            rhs_scale=a_scales[:, nodes],
-                            start=(g == 0),
-                            stop=(g == NODE_PASSES - 1),
-                        )
-                cols = slice(c * P * PACK, (c + 1) * P * PACK)
-                nc.vector.scalar_tensor_tensor(
-                    out=z_grouped[:, cols].rearrange("p (n t) -> p n t", t=PACK),
-                    in0=hT_sb[:, cols].rearrange("p (n t) -> p n t", t=PACK),
-                    scalar=self_w[:, 0:1],
-                    in1=z_bank[:].rearrange("p t n -> p n t"),
-                    op0=ALU.mult,
-                    op1=ALU.add,
-                )
-            nc.vector.quantize_mx(
-                out=z_codes[:, h * 2 * P : (h + 1) * 2 * P].bitcast(FP8X4),
-                scales=z_scales[:, h * 2 * P : (h + 1) * 2 * P],
-                in_=z_grouped[:, h * 2 * P * PACK : (h + 1) * 2 * P * PACK],
-            )
-
-        def linear_relu_store(h):
-            for c in (2 * h, 2 * h + 1):
-                o_bank = psum_o.tile([P, HID], F32)
-                nc.tensor.matmul_mx(
-                    out=o_bank[:],
-                    lhsT=z_codes[:, c * P : (c + 1) * P].bitcast(FP8X4),
-                    lhsT_scale=z_scales[:, c * P : (c + 1) * P],
-                    rhs=w_codes[:].bitcast(FP8X4),
-                    rhs_scale=w_scales[:],
-                    start=True,
-                    stop=True,
-                )
-                nc.vector.tensor_tensor(
-                    out=o_sum[:, c * HID : (c + 1) * HID], in0=o_bank[:], in1=b_all[:], op=ALU.add
-                )
-            both = slice(h * 2 * HID, (h + 1) * 2 * HID)
-            nc.scalar.activation(out=o_sb[:, both], in_=o_sum[:, both], func=ACT.Relu)
-            nc.sync.dma_start(out=out_rows[:, h, :], in_=o_sb[:, both])
-
-        for step in range(PAIRS + 2):
-            if step < PAIRS:
-                transpose_and_quantise_a(step)
-            if 1 <= step <= PAIRS:
-                aggregate_and_quantise_z(step - 1)
-            if step >= 2:
-                linear_relu_store(step - 2)
+            if 0 <= step - LAG_LINEAR < CHUNKS:
+                linear(step - LAG_LINEAR)
+            if step < 2:
+                transpose_a(4 + 2 * step)
+                transpose_a(5 + 2 * step)
+            if step < CHUNKS:
+                add_self_term(step)
+            if step + 2 < CHUNKS:
+                quantise_a(step + 2)
+            if step < CHUNKS:
+                quantise_z(step)
+            if step >= LAG_BIAS:
+                bias_relu_store(step - LAG_BIAS)

@@ -22,11 +22,15 @@ PAIRS = CHUNKS // 2
 ROW_WORDS = NODES // 2
 HID_WORDS = HID // 2
 
+AHEAD_TRANSPOSE = 5
+AHEAD_QUANTISE = 3
+AHEAD_AGGREGATE = 1
+BEHIND_LINEAR = 2
+BEHIND_BIAS = 3
+A_CHUNKS_BEFORE_W = 6
+W_REGROUP_BEHIND_CHUNK = 4
+
 FLOPS = 2 * NODES * NODES * HID + 2 * NODES * HID * HID
-
-
-LAG_LINEAR = 2
-LAG_BIAS = 3
 
 
 def tile_gin_pb_kernel(tc, A, h1, eps1, W1_1, b1_1, out):
@@ -65,40 +69,39 @@ def tile_gin_pb_kernel(tc, A, h1, eps1, W1_1, b1_1, out):
         b_all = keep.tile([P, HID], F32)
         eps_col = keep.tile([P, 1], BF16)
         self_w = keep.tile([P, 1], F32)
+        warm = keep.tile([P, 1], F32)
+
+        a_rows = A.rearrange("(h p e) k -> p h e k", h=PAIRS, e=2)
+
+        def load_a(c):
+            nc.sync.dma_start(
+                out=a_sb[:, c * NODES : (c + 1) * NODES], in_=a_rows[:, c // 2, c % 2, :]
+            )
 
         nc.vector.memset(b_rows[:], 0.0)
-        nc.sync.dma_start(out=b_rows[0:1, :], in_=b1_1.rearrange("(r o) -> r o", r=1))
         with nc.allow_non_contiguous_dma(reason="one bfloat16 scalar to every partition"):
             nc.sync.dma_start(out=eps_col[:], in_=eps1.partition_broadcast(P))
-
-        def load_h1(h):
+        for h in range(PAIRS):
             nc.sync.dma_start(
                 out=h1_sb[:, h * 2 * HID : (h + 1) * 2 * HID],
                 in_=h1[h * 2 * P : (h + 1) * 2 * P, :].rearrange("(p e) f -> p (e f)", e=2),
             )
-
-        def load_a(h):
-            nc.sync.dma_start(
-                out=a_sb[:, h * 2 * NODES : (h + 1) * 2 * NODES],
-                in_=A[h * 2 * P : (h + 1) * 2 * P, :].rearrange("(p e) k -> p (e k)", e=2),
-            )
-
-        for h in range(PAIRS):
-            load_h1(h)
-        load_a(0)
-        load_a(1)
+        nc.sync.dma_start(out=b_rows[0:1, :], in_=b1_1.rearrange("(r o) -> r o", r=1))
+        for c in range(A_CHUNKS_BEFORE_W):
+            load_a(c)
         nc.sync.dma_start(
             out=w_sb[:].rearrange("p (v r) -> p v r", v=2),
             in_=W1_1.rearrange("(v p e) o -> p v (e o)", v=2, e=2),
         )
-        load_a(2)
-        load_a(3)
+        for c in range(A_CHUNKS_BEFORE_W, CHUNKS):
+            load_a(c)
 
         make_identity(nc, ident[:])
         nc.vector.memset(ones[:], 1.0)
         nc.vector.tensor_scalar(
             out=self_w[:], in0=eps_col[:], scalar1=1.0, scalar2=None, op0=ALU.add
         )
+        nc.scalar.activation(out=warm[:], in_=ones[:, 0:1], func=ACT.Relu)
 
         h1_rows = h1_sb[:].rearrange(
             "p (g t v q e) -> p g v q t e", g=NODE_PASSES, t=PACK, v=2, e=2
@@ -217,37 +220,33 @@ def tile_gin_pb_kernel(tc, A, h1, eps1, W1_1, b1_1, out):
         regroup_h1(1, 0)
         quantise_h1(0)
         regroup_h1(1, 1)
-        for c in range(4):
-            transpose_a(c)
-        quantise_a(0)
         quantise_h1(1)
-        quantise_a(1)
-        aggregate(0)
-        b_bank = psum_t.tile([P, HID], F32, tag="t")
+        b_bank = psum_o.tile([P, HID], F32, name="o_bank")
         nc.tensor.matmul(out=b_bank[:], lhsT=ones[:], rhs=b_rows[:], start=True, stop=True)
-        nc.scalar.copy(out=b_all[:], in_=b_bank[:])
-        nc.scalar.copy(
-            out=w_grouped[:].rearrange("p (c i t) -> p c t i", i=4, t=PACK),
-            in_=w_sb[:].rearrange("p (t c i) -> p c t i", t=PACK, i=4),
-        )
 
-        for step in range(CHUNKS + LAG_BIAS):
-            if step + 1 < CHUNKS:
-                aggregate(step + 1)
-            if step == LAG_LINEAR:
+        for step in range(-AHEAD_TRANSPOSE, CHUNKS + BEHIND_BIAS):
+            entering = step + AHEAD_TRANSPOSE
+            if entering < CHUNKS:
+                transpose_a(entering)
+            if entering == W_REGROUP_BEHIND_CHUNK:
+                nc.scalar.copy(
+                    out=w_grouped[:].rearrange("p (c i t) -> p c t i", i=4, t=PACK),
+                    in_=w_sb[:].rearrange("p (t c i) -> p c t i", t=PACK, i=4),
+                )
+                nc.scalar.copy(out=b_all[:], in_=b_bank[:])
+            if 0 <= step + AHEAD_AGGREGATE < CHUNKS:
+                aggregate(step + AHEAD_AGGREGATE)
+            if step == BEHIND_LINEAR:
                 nc.vector.quantize_mx(
                     out=w_codes[:].bitcast(FP8X4), scales=w_scales[:], in_=w_grouped[:]
                 )
-            if 0 <= step - LAG_LINEAR < CHUNKS:
-                linear(step - LAG_LINEAR)
-            if step < 2:
-                transpose_a(4 + 2 * step)
-                transpose_a(5 + 2 * step)
-            if step < CHUNKS:
+            if 0 <= step - BEHIND_LINEAR < CHUNKS:
+                linear(step - BEHIND_LINEAR)
+            if 0 <= step < CHUNKS:
                 add_self_term(step)
-            if step + 2 < CHUNKS:
-                quantise_a(step + 2)
-            if step < CHUNKS:
+            if 0 <= step + AHEAD_QUANTISE < CHUNKS:
+                quantise_a(step + AHEAD_QUANTISE)
+            if 0 <= step < CHUNKS:
                 quantise_z(step)
-            if step >= LAG_BIAS:
-                bias_relu_store(step - LAG_BIAS)
+            if step >= BEHIND_BIAS:
+                bias_relu_store(step - BEHIND_BIAS)

@@ -25,6 +25,7 @@ HID_WORDS = HID // 2
 AHEAD_TRANSPOSE = 5
 AHEAD_QUANTISE = 3
 AHEAD_AGGREGATE = 1
+BEHIND_QUANTISE_Z = 1
 BEHIND_LINEAR = 2
 BEHIND_BIAS = 3
 A_CHUNKS_BEFORE_W = 6
@@ -79,13 +80,13 @@ def tile_gin_pb_kernel(tc, A, h1, eps1, W1_1, b1_1, out):
             )
 
         nc.vector.memset(b_rows[:], 0.0)
-        with nc.allow_non_contiguous_dma(reason="one bfloat16 scalar to every partition"):
-            nc.sync.dma_start(out=eps_col[:], in_=eps1.partition_broadcast(P))
         for h in range(PAIRS):
             nc.sync.dma_start(
                 out=h1_sb[:, h * 2 * HID : (h + 1) * 2 * HID],
                 in_=h1[h * 2 * P : (h + 1) * 2 * P, :].rearrange("(p e) f -> p (e f)", e=2),
             )
+        with nc.allow_non_contiguous_dma(reason="one bfloat16 scalar to every partition"):
+            nc.sync.dma_start(out=eps_col[:], in_=eps1.partition_broadcast(P))
         nc.sync.dma_start(out=b_rows[0:1, :], in_=b1_1.rearrange("(r o) -> r o", r=1))
         for c in range(A_CHUNKS_BEFORE_W):
             load_a(c)
@@ -98,9 +99,6 @@ def tile_gin_pb_kernel(tc, A, h1, eps1, W1_1, b1_1, out):
 
         make_identity(nc, ident[:])
         nc.vector.memset(ones[:], 1.0)
-        nc.vector.tensor_scalar(
-            out=self_w[:], in0=eps_col[:], scalar1=1.0, scalar2=None, op0=ALU.add
-        )
         nc.scalar.activation(out=warm[:], in_=ones[:, 0:1], func=ACT.Relu)
 
         h1_rows = h1_sb[:].rearrange(
@@ -218,9 +216,12 @@ def tile_gin_pb_kernel(tc, A, h1, eps1, W1_1, b1_1, out):
         regroup_h1(0, 0)
         regroup_h1(0, 1)
         regroup_h1(1, 0)
-        quantise_h1(0)
         regroup_h1(1, 1)
+        quantise_h1(0)
         quantise_h1(1)
+        nc.vector.tensor_scalar(
+            out=self_w[:], in0=eps_col[:], scalar1=1.0, scalar2=None, op0=ALU.add
+        )
         b_bank = psum_o.tile([P, HID], F32, name="o_bank")
         nc.tensor.matmul(out=b_bank[:], lhsT=ones[:], rhs=b_rows[:], start=True, stop=True)
 
@@ -246,7 +247,7 @@ def tile_gin_pb_kernel(tc, A, h1, eps1, W1_1, b1_1, out):
                 add_self_term(step)
             if 0 <= step + AHEAD_QUANTISE < CHUNKS:
                 quantise_a(step + AHEAD_QUANTISE)
-            if 0 <= step < CHUNKS:
-                quantise_z(step)
+            if 0 <= step - BEHIND_QUANTISE_Z < CHUNKS:
+                quantise_z(step - BEHIND_QUANTISE_Z)
             if step >= BEHIND_BIAS:
                 bias_relu_store(step - BEHIND_BIAS)

@@ -67,6 +67,7 @@ def tile_gin_pb_kernel(tc, A, h1, eps1, W1_1, b1_1, out):
         ident = keep.tile([P, P], F32)
         ones = keep.tile([P, P], BF16)
         b_rows = keep.tile([P, HID], BF16)
+        zeros = keep.tile([P, HID], BF16)
         b_all = keep.tile([P, HID], F32)
         eps_col = keep.tile([P, 1], BF16)
         self_w = keep.tile([P, 1], F32)
@@ -97,8 +98,9 @@ def tile_gin_pb_kernel(tc, A, h1, eps1, W1_1, b1_1, out):
         for c in range(A_CHUNKS_BEFORE_W, CHUNKS):
             load_a(c)
 
-        make_identity(nc, ident[:])
         nc.vector.memset(ones[:], 1.0)
+        nc.vector.memset(zeros[:], 0.0)
+        make_identity(nc, ident[:])
         nc.scalar.activation(out=warm[:], in_=ones[:, 0:1], func=ACT.Relu)
 
         h1_rows = h1_sb[:].rearrange(
@@ -159,6 +161,14 @@ def tile_gin_pb_kernel(tc, A, h1, eps1, W1_1, b1_1, out):
         z_banks = {}
         o_banks = {}
 
+        idle_bank = psum_o.tile([P, HID], F32, name="o_bank")
+
+        def keep_clock_up(times):
+            for i in range(times):
+                nc.tensor.matmul(
+                    out=idle_bank[:], lhsT=ones[:], rhs=zeros[:], start=True, stop=True
+                )
+
         def aggregate(c):
             z_banks[c] = psum_z.tile([P, PACK, P], F32, name="z_bank")
             for t in range(PACK):
@@ -211,8 +221,12 @@ def tile_gin_pb_kernel(tc, A, h1, eps1, W1_1, b1_1, out):
             nc.scalar.activation(out=o_sb[:, cols], in_=o_sum[:, cols], func=ACT.Relu)
             nc.sync.dma_start(out=out_rows[:, c // 2, c % 2, :], in_=o_sb[:, cols])
 
+        keep_clock_up(4)
+
         for h in range(PAIRS):
             transpose_h1(h)
+            if h % 2 == 0:
+                keep_clock_up(1)
         regroup_h1(0, 0)
         regroup_h1(0, 1)
         regroup_h1(1, 0)
@@ -229,6 +243,8 @@ def tile_gin_pb_kernel(tc, A, h1, eps1, W1_1, b1_1, out):
             entering = step + AHEAD_TRANSPOSE
             if entering < CHUNKS:
                 transpose_a(entering)
+                if entering in (1, 3):
+                    keep_clock_up(1)
             if entering == W_REGROUP_BEHIND_CHUNK:
                 nc.scalar.copy(
                     out=w_grouped[:].rearrange("p (c i t) -> p c t i", i=4, t=PACK),

@@ -22,14 +22,11 @@ PAIRS = CHUNKS // 2
 ROW_WORDS = NODES // 2
 HID_WORDS = HID // 2
 
-AHEAD_TRANSPOSE = 5
-AHEAD_QUANTISE = 3
-AHEAD_AGGREGATE = 1
+AHEAD_TRANSPOSE = 4
+AHEAD_QUANTISE = 2
 BEHIND_QUANTISE_Z = 1
-BEHIND_LINEAR = 2
-BEHIND_BIAS = 3
-A_CHUNKS_BEFORE_W = 6
-W_REGROUP_BEHIND_CHUNK = 4
+BEHIND_BIAS = 4
+A_CHUNKS_BEFORE_W = 4
 
 FLOPS = 2 * NODES * NODES * HID + 2 * NODES * HID * HID
 
@@ -66,9 +63,8 @@ def tile_gin_pb_kernel(tc, A, h1, eps1, W1_1, b1_1, out):
 
         ident = keep.tile([P, P], F32)
         ones = keep.tile([P, P], BF16)
-        b_rows = keep.tile([P, HID], BF16)
         zeros = keep.tile([P, HID], BF16)
-        b_all = keep.tile([P, HID], F32)
+        b_all = keep.tile([P, HID], BF16)
         eps_col = keep.tile([P, 1], BF16)
         self_w = keep.tile([P, 1], F32)
         warm = keep.tile([P, 1], F32)
@@ -80,7 +76,6 @@ def tile_gin_pb_kernel(tc, A, h1, eps1, W1_1, b1_1, out):
                 out=a_sb[:, c * NODES : (c + 1) * NODES], in_=a_rows[:, c // 2, c % 2, :]
             )
 
-        nc.vector.memset(b_rows[:], 0.0)
         for h in range(PAIRS):
             nc.sync.dma_start(
                 out=h1_sb[:, h * 2 * HID : (h + 1) * 2 * HID],
@@ -88,7 +83,6 @@ def tile_gin_pb_kernel(tc, A, h1, eps1, W1_1, b1_1, out):
             )
         with nc.allow_non_contiguous_dma(reason="one bfloat16 scalar to every partition"):
             nc.sync.dma_start(out=eps_col[:], in_=eps1.partition_broadcast(P))
-        nc.sync.dma_start(out=b_rows[0:1, :], in_=b1_1.rearrange("(r o) -> r o", r=1))
         for c in range(A_CHUNKS_BEFORE_W):
             load_a(c)
         nc.sync.dma_start(
@@ -97,9 +91,10 @@ def tile_gin_pb_kernel(tc, A, h1, eps1, W1_1, b1_1, out):
         )
         for c in range(A_CHUNKS_BEFORE_W, CHUNKS):
             load_a(c)
+        nc.sync.dma_start(out=b_all[:], in_=b1_1.partition_broadcast(P))
 
-        nc.vector.memset(ones[:], 1.0)
         nc.vector.memset(zeros[:], 0.0)
+        nc.vector.memset(ones[:], 1.0)
         make_identity(nc, ident[:])
         nc.scalar.activation(out=warm[:], in_=ones[:, 0:1], func=ACT.Relu)
 
@@ -115,19 +110,25 @@ def tile_gin_pb_kernel(tc, A, h1, eps1, W1_1, b1_1, out):
         a_slots = a_grouped[:].bitcast(F32).rearrange(
             "p (c g n u) -> p c g n u", c=CHUNKS, g=NODE_PASSES, u=2
         )
+        w_rows = w_sb[:].rearrange("p (t o) -> p t o", t=PACK)
+        w_slots = w_grouped[:].rearrange("p (o t) -> p o t", t=PACK)
         out_rows = out.rearrange("(h p e) o -> p h e o", h=PAIRS, e=2)
 
-        def transpose_h1(h):
-            hT_bank = psum_t.tile([P, 2, 2, P], F32, tag="t")
+        h_banks = {}
+
+        def transpose_h1(h, pool, tag):
+            h_banks[h] = pool.tile([P, 2, 2, P], F32, name="hT_bank", tag=tag)
             for i in range(2):
                 for v in range(2):
                     first = (2 * h + i) * HID_WORDS + v * P
                     nc.tensor.transpose(
-                        hT_bank[:, i, v, :], h1_words[:, first : first + P], ident[:]
+                        h_banks[h][:, i, v, :], h1_words[:, first : first + P], ident[:]
                     )
+
+        def copy_h1_transposed(h):
             nc.scalar.copy(
                 out=hT_words[:, 2 * h : 2 * h + 2],
-                in_=hT_bank[:].rearrange("p i v n -> p i n v"),
+                in_=h_banks[h][:].rearrange("p i v n -> p i n v"),
             )
 
         def regroup_h1(g, v):
@@ -138,6 +139,13 @@ def tile_gin_pb_kernel(tc, A, h1, eps1, W1_1, b1_1, out):
                 out=h_codes[:, g * HID : (g + 1) * HID].bitcast(FP8X4),
                 scales=h_scales[:, g * HID : (g + 1) * HID],
                 in_=h_grouped[:, g * HID * PACK : (g + 1) * HID * PACK],
+            )
+
+        def regroup_w(quarter):
+            outs = slice(quarter * P, (quarter + 1) * P)
+            nc.scalar.copy(
+                out=w_slots[:, outs].rearrange("p (c i) t -> p c t i", i=4),
+                in_=w_rows[:, :, outs].rearrange("p t (c i) -> p c t i", i=4),
             )
 
         def transpose_a(c):
@@ -161,16 +169,8 @@ def tile_gin_pb_kernel(tc, A, h1, eps1, W1_1, b1_1, out):
         z_banks = {}
         o_banks = {}
 
-        idle_bank = psum_o.tile([P, HID], F32, name="o_bank")
-
-        def keep_clock_up(times):
-            for i in range(times):
-                nc.tensor.matmul(
-                    out=idle_bank[:], lhsT=ones[:], rhs=zeros[:], start=True, stop=True
-                )
-
         def aggregate(c):
-            z_banks[c] = psum_z.tile([P, PACK, P], F32, name="z_bank")
+            z_banks[c] = psum_z.tile([P, PACK, P], F32, name="z_bank", tag="z_bank")
             for t in range(PACK):
                 for g in range(NODE_PASSES):
                     feats = slice(g * HID + t * P, g * HID + (t + 1) * P)
@@ -204,7 +204,7 @@ def tile_gin_pb_kernel(tc, A, h1, eps1, W1_1, b1_1, out):
             )
 
         def linear(c):
-            o_banks[c] = psum_o.tile([P, HID], F32, name="o_bank")
+            o_banks[c] = psum_o.tile([P, HID], F32, name="o_bank", tag="o_bank")
             nc.tensor.matmul_mx(
                 out=o_banks[c][:],
                 lhsT=z_codes[:, c * P : (c + 1) * P].bitcast(FP8X4),
@@ -221,47 +221,64 @@ def tile_gin_pb_kernel(tc, A, h1, eps1, W1_1, b1_1, out):
             nc.scalar.activation(out=o_sb[:, cols], in_=o_sum[:, cols], func=ACT.Relu)
             nc.sync.dma_start(out=out_rows[:, c // 2, c % 2, :], in_=o_sb[:, cols])
 
-        keep_clock_up(4)
+        head_bank = psum_z.tile([P, HID], F32, name="head_bank", tag="z_bank")
 
-        for h in range(PAIRS):
-            transpose_h1(h)
-            if h % 2 == 0:
-                keep_clock_up(1)
+        def keep_clock_up(times):
+            for i in range(times):
+                nc.tensor.matmul(
+                    out=head_bank[:], lhsT=ones[:], rhs=zeros[:], start=True, stop=True
+                )
+
+        keep_clock_up(4)
+        transpose_h1(0, psum_t, "t")
+        transpose_h1(1, psum_z, "z_bank")
+        keep_clock_up(1)
+        transpose_h1(2, psum_o, "o_bank")
+        transpose_h1(3, psum_o, "o_bank")
+        keep_clock_up(1)
+        copy_h1_transposed(0)
+        copy_h1_transposed(1)
         regroup_h1(0, 0)
         regroup_h1(0, 1)
         regroup_h1(1, 0)
-        regroup_h1(1, 1)
+        nc.scalar.copy(out=h_slots[:, 1, 1], in_=h1_rows[:, 1, 1])
         quantise_h1(0)
         quantise_h1(1)
         nc.vector.tensor_scalar(
             out=self_w[:], in0=eps_col[:], scalar1=1.0, scalar2=None, op0=ALU.add
         )
-        b_bank = psum_o.tile([P, HID], F32, name="o_bank")
-        nc.tensor.matmul(out=b_bank[:], lhsT=ones[:], rhs=b_rows[:], start=True, stop=True)
+        for c in range(PAIRS):
+            transpose_a(c)
+            if c < 3:
+                keep_clock_up(1)
+        for c in range(3):
+            quantise_a(c)
 
-        for step in range(-AHEAD_TRANSPOSE, CHUNKS + BEHIND_BIAS):
-            entering = step + AHEAD_TRANSPOSE
-            if entering < CHUNKS:
-                transpose_a(entering)
-                if entering in (1, 3):
-                    keep_clock_up(1)
-            if entering == W_REGROUP_BEHIND_CHUNK:
-                nc.scalar.copy(
-                    out=w_grouped[:].rearrange("p (c i t) -> p c t i", i=4, t=PACK),
-                    in_=w_sb[:].rearrange("p (t c i) -> p c t i", t=PACK, i=4),
-                )
-                nc.scalar.copy(out=b_all[:], in_=b_bank[:])
-            if 0 <= step + AHEAD_AGGREGATE < CHUNKS:
-                aggregate(step + AHEAD_AGGREGATE)
-            if step == BEHIND_LINEAR:
-                nc.vector.quantize_mx(
-                    out=w_codes[:].bitcast(FP8X4), scales=w_scales[:], in_=w_grouped[:]
-                )
-            if 0 <= step - BEHIND_LINEAR < CHUNKS:
-                linear(step - BEHIND_LINEAR)
-            if 0 <= step < CHUNKS:
+        for step in range(CHUNKS + BEHIND_BIAS):
+            if step % 2 == 0:
+                if step == BEHIND_BIAS:
+                    nc.vector.quantize_mx(
+                        out=w_codes[:].bitcast(FP8X4), scales=w_scales[:], in_=w_grouped[:]
+                    )
+                for c in (step, step + 1):
+                    if c < CHUNKS:
+                        aggregate(c)
+                    if 0 <= c - BEHIND_BIAS < CHUNKS:
+                        linear(c - BEHIND_BIAS)
+                if step + AHEAD_TRANSPOSE < CHUNKS:
+                    regroup_w(step)
+                    regroup_w(step + 1)
+                    if step > 0:
+                        copy_h1_transposed(2)
+                    transpose_a(step + AHEAD_TRANSPOSE)
+                    transpose_a(step + AHEAD_TRANSPOSE + 1)
+                    if step > 0:
+                        copy_h1_transposed(3)
+            if step < CHUNKS:
                 add_self_term(step)
-            if 0 <= step + AHEAD_QUANTISE < CHUNKS:
+            if step == 0:
+                quantise_a(3)
+            elif 4 <= step + AHEAD_QUANTISE < CHUNKS:
                 quantise_a(step + AHEAD_QUANTISE)
             if 0 <= step - BEHIND_QUANTISE_Z < CHUNKS:
                 quantise_z(step - BEHIND_QUANTISE_Z)

@@ -26,7 +26,6 @@ AHEAD_TRANSPOSE = 4
 AHEAD_QUANTISE = 2
 BEHIND_QUANTISE_Z = 1
 BEHIND_BIAS = 4
-A_CHUNKS_BEFORE_W = 4
 
 FLOPS = 2 * NODES * NODES * HID + 2 * NODES * HID * HID
 
@@ -64,8 +63,8 @@ def tile_gin_pb_kernel(tc, A, h1, eps1, W1_1, b1_1, out):
         ident = keep.tile([P, P], F32)
         ones = keep.tile([P, P], BF16)
         zeros = keep.tile([P, HID], BF16)
-        b_all = keep.tile([P, HID], BF16)
-        eps_col = keep.tile([P, 1], BF16)
+        rows = keep.tile([P, HID + 16], BF16)
+        b_all = keep.tile([P, HID], F32)
         self_w = keep.tile([P, 1], F32)
         warm = keep.tile([P, 1], F32)
 
@@ -76,24 +75,36 @@ def tile_gin_pb_kernel(tc, A, h1, eps1, W1_1, b1_1, out):
                 out=a_sb[:, c * NODES : (c + 1) * NODES], in_=a_rows[:, c // 2, c % 2, :]
             )
 
+        def load_a_pair(h):
+            nc.sync.dma_start(
+                out=a_sb[:, 2 * h * NODES : 2 * (h + 1) * NODES],
+                in_=A[h * 2 * P : (h + 1) * 2 * P, :].rearrange("(p e) k -> p (e k)", e=2),
+            )
+
+        nc.vector.memset(rows[:].bitcast(U32), 0)
         for h in range(PAIRS):
+            if h == 1:
+                nc.sync.dma_start(
+                    out=rows[0:1, 0:HID], in_=b1_1.rearrange("(r o) -> r o", r=1)
+                )
+                nc.sync.dma_start(
+                    out=rows[0:1, HID : HID + 1], in_=eps1.rearrange("(r o) -> r o", r=1)
+                )
             nc.sync.dma_start(
                 out=h1_sb[:, h * 2 * HID : (h + 1) * 2 * HID],
                 in_=h1[h * 2 * P : (h + 1) * 2 * P, :].rearrange("(p e) f -> p (e f)", e=2),
             )
-        with nc.allow_non_contiguous_dma(reason="one bfloat16 scalar to every partition"):
-            nc.sync.dma_start(out=eps_col[:], in_=eps1.partition_broadcast(P))
-        for c in range(A_CHUNKS_BEFORE_W):
-            load_a(c)
+        load_a(0)
+        load_a(1)
+        load_a_pair(1)
         nc.sync.dma_start(
             out=w_sb[:].rearrange("p (v r) -> p v r", v=2),
             in_=W1_1.rearrange("(v p e) o -> p v (e o)", v=2, e=2),
         )
-        for c in range(A_CHUNKS_BEFORE_W, CHUNKS):
-            load_a(c)
-        nc.sync.dma_start(out=b_all[:], in_=b1_1.partition_broadcast(P))
+        load_a_pair(2)
+        load_a_pair(3)
 
-        nc.vector.memset(zeros[:], 0.0)
+        nc.vector.memset(zeros[:].bitcast(U32), 0)
         nc.vector.memset(ones[:], 1.0)
         make_identity(nc, ident[:])
         nc.scalar.activation(out=warm[:], in_=ones[:, 0:1], func=ACT.Relu)
@@ -216,10 +227,19 @@ def tile_gin_pb_kernel(tc, A, h1, eps1, W1_1, b1_1, out):
             )
 
         def bias_relu_store(c):
-            cols = slice(c * HID, (c + 1) * HID)
-            nc.vector.tensor_tensor(out=o_sum[:, cols], in0=o_banks[c][:], in1=b_all[:], op=ALU.add)
-            nc.scalar.activation(out=o_sb[:, cols], in_=o_sum[:, cols], func=ACT.Relu)
-            nc.sync.dma_start(out=out_rows[:, c // 2, c % 2, :], in_=o_sb[:, cols])
+            width = HID // 2 if c == CHUNKS - 1 else HID
+            for o in range(0, HID, width):
+                cols = slice(c * HID + o, c * HID + o + width)
+                nc.vector.tensor_tensor(
+                    out=o_sum[:, cols],
+                    in0=o_banks[c][:, o : o + width],
+                    in1=b_all[:, o : o + width],
+                    op=ALU.add,
+                )
+                nc.scalar.activation(out=o_sb[:, cols], in_=o_sum[:, cols], func=ACT.Relu)
+                nc.sync.dma_start(
+                    out=out_rows[:, c // 2, c % 2, o : o + width], in_=o_sb[:, cols]
+                )
 
         head_bank = psum_z.tile([P, HID], F32, name="head_bank", tag="z_bank")
 
@@ -235,6 +255,10 @@ def tile_gin_pb_kernel(tc, A, h1, eps1, W1_1, b1_1, out):
         keep_clock_up(1)
         transpose_h1(2, psum_o, "o_bank")
         transpose_h1(3, psum_o, "o_bank")
+        eps_bank = psum_t.tile([P, 16], F32, name="eps_bank", tag="t")
+        nc.tensor.matmul(
+            out=eps_bank[:], lhsT=ones[:], rhs=rows[:, HID : HID + 16], start=True, stop=True
+        )
         keep_clock_up(1)
         copy_h1_transposed(0)
         copy_h1_transposed(1)
@@ -242,14 +266,14 @@ def tile_gin_pb_kernel(tc, A, h1, eps1, W1_1, b1_1, out):
         regroup_h1(0, 1)
         regroup_h1(1, 0)
         nc.scalar.copy(out=h_slots[:, 1, 1], in_=h1_rows[:, 1, 1])
+        nc.vector.tensor_scalar(
+            out=self_w[:], in0=eps_bank[:, 0:1], scalar1=1.0, scalar2=None, op0=ALU.add
+        )
         quantise_h1(0)
         quantise_h1(1)
-        nc.vector.tensor_scalar(
-            out=self_w[:], in0=eps_col[:], scalar1=1.0, scalar2=None, op0=ALU.add
-        )
         for c in range(PAIRS):
             transpose_a(c)
-            if c < 3:
+            if c < 2:
                 keep_clock_up(1)
         for c in range(3):
             quantise_a(c)
@@ -270,6 +294,11 @@ def tile_gin_pb_kernel(tc, A, h1, eps1, W1_1, b1_1, out):
                     regroup_w(step + 1)
                     if step > 0:
                         copy_h1_transposed(2)
+                        b_bank = psum_t.tile([P, HID], F32, name="b_bank", tag="t")
+                        nc.tensor.matmul(
+                            out=b_bank[:], lhsT=ones[:], rhs=rows[:, 0:HID], start=True, stop=True
+                        )
+                        nc.scalar.copy(out=b_all[:], in_=b_bank[:])
                     transpose_a(step + AHEAD_TRANSPOSE)
                     transpose_a(step + AHEAD_TRANSPOSE + 1)
                     if step > 0:

@@ -81,21 +81,20 @@ def tile_gin_pb_kernel(tc, A, h1, eps1, W1_1, b1_1, out):
                 in_=A[h * 2 * P : (h + 1) * 2 * P, :].rearrange("(p e) k -> p (e k)", e=2),
             )
 
+        nc.vector.memset(zeros[:].bitcast(U32), 0)
+        nc.vector.memset(ones[:], 1.0)
         nc.vector.memset(rows[:].bitcast(U32), 0)
         for h in range(PAIRS):
-            if h == 1:
-                nc.sync.dma_start(
-                    out=rows[0:1, 0:HID], in_=b1_1.rearrange("(r o) -> r o", r=1)
-                )
-                nc.sync.dma_start(
-                    out=rows[0:1, HID : HID + 1], in_=eps1.rearrange("(r o) -> r o", r=1)
-                )
             nc.sync.dma_start(
                 out=h1_sb[:, h * 2 * HID : (h + 1) * 2 * HID],
                 in_=h1[h * 2 * P : (h + 1) * 2 * P, :].rearrange("(p e) f -> p (e f)", e=2),
             )
         load_a(0)
         load_a(1)
+        nc.sync.dma_start(
+            out=rows[0:1, HID : HID + 1], in_=eps1.rearrange("(r o) -> r o", r=1)
+        )
+        nc.sync.dma_start(out=rows[0:1, 0:HID], in_=b1_1.rearrange("(r o) -> r o", r=1))
         load_a_pair(1)
         nc.sync.dma_start(
             out=w_sb[:].rearrange("p (v r) -> p v r", v=2),
@@ -104,8 +103,6 @@ def tile_gin_pb_kernel(tc, A, h1, eps1, W1_1, b1_1, out):
         load_a_pair(2)
         load_a_pair(3)
 
-        nc.vector.memset(zeros[:].bitcast(U32), 0)
-        nc.vector.memset(ones[:], 1.0)
         make_identity(nc, ident[:])
         nc.scalar.activation(out=warm[:], in_=ones[:, 0:1], func=ACT.Relu)
 
@@ -255,10 +252,6 @@ def tile_gin_pb_kernel(tc, A, h1, eps1, W1_1, b1_1, out):
         keep_clock_up(1)
         transpose_h1(2, psum_o, "o_bank")
         transpose_h1(3, psum_o, "o_bank")
-        eps_bank = psum_t.tile([P, 16], F32, name="eps_bank", tag="t")
-        nc.tensor.matmul(
-            out=eps_bank[:], lhsT=ones[:], rhs=rows[:, HID : HID + 16], start=True, stop=True
-        )
         keep_clock_up(1)
         copy_h1_transposed(0)
         copy_h1_transposed(1)
@@ -266,17 +259,27 @@ def tile_gin_pb_kernel(tc, A, h1, eps1, W1_1, b1_1, out):
         regroup_h1(0, 1)
         regroup_h1(1, 0)
         nc.scalar.copy(out=h_slots[:, 1, 1], in_=h1_rows[:, 1, 1])
-        nc.vector.tensor_scalar(
-            out=self_w[:], in0=eps_bank[:, 0:1], scalar1=1.0, scalar2=None, op0=ALU.add
-        )
         quantise_h1(0)
         quantise_h1(1)
         for c in range(PAIRS):
             transpose_a(c)
             if c < 2:
                 keep_clock_up(1)
+            if c == 1:
+                eps_bank = psum_t.tile([P, 16], F32, name="eps_bank", tag="t")
+                nc.tensor.matmul(
+                    out=eps_bank[:],
+                    lhsT=ones[:],
+                    rhs=rows[:, HID : HID + 16],
+                    start=True,
+                    stop=True,
+                )
         for c in range(3):
             quantise_a(c)
+            if c == 1:
+                nc.vector.tensor_scalar(
+                    out=self_w[:], in0=eps_bank[:, 0:1], scalar1=1.0, scalar2=None, op0=ALU.add
+                )
 
         for step in range(CHUNKS + BEHIND_BIAS):
             if step % 2 == 0:
@@ -292,17 +295,18 @@ def tile_gin_pb_kernel(tc, A, h1, eps1, W1_1, b1_1, out):
                 if step + AHEAD_TRANSPOSE < CHUNKS:
                     regroup_w(step)
                     regroup_w(step + 1)
-                    if step > 0:
-                        copy_h1_transposed(2)
-                        b_bank = psum_t.tile([P, HID], F32, name="b_bank", tag="t")
-                        nc.tensor.matmul(
-                            out=b_bank[:], lhsT=ones[:], rhs=rows[:, 0:HID], start=True, stop=True
-                        )
-                        nc.scalar.copy(out=b_all[:], in_=b_bank[:])
+                if step == 2:
+                    copy_h1_transposed(2)
+                    b_bank = psum_t.tile([P, HID], F32, name="b_bank", tag="t")
+                    nc.tensor.matmul(
+                        out=b_bank[:], lhsT=ones[:], rhs=rows[:, 0:HID], start=True, stop=True
+                    )
+                    nc.scalar.copy(out=b_all[:], in_=b_bank[:])
+                if step + AHEAD_TRANSPOSE < CHUNKS:
                     transpose_a(step + AHEAD_TRANSPOSE)
                     transpose_a(step + AHEAD_TRANSPOSE + 1)
-                    if step > 0:
-                        copy_h1_transposed(3)
+                if step == 2:
+                    copy_h1_transposed(3)
             if step < CHUNKS:
                 add_self_term(step)
             if step == 0:

@@ -22,10 +22,7 @@ PAIRS = CHUNKS // 2
 ROW_WORDS = NODES // 2
 HID_WORDS = HID // 2
 
-AHEAD_TRANSPOSE = 4
-AHEAD_QUANTISE = 2
-BEHIND_QUANTISE_Z = 1
-BEHIND_BIAS = 4
+HALF = CHUNKS // 2
 
 FLOPS = 2 * NODES * NODES * HID + 2 * NODES * HID * HID
 
@@ -36,7 +33,7 @@ def tile_gin_pb_kernel(tc, A, h1, eps1, W1_1, b1_1, out):
         keep = ctx.enter_context(tc.tile_pool(name="keep", bufs=1))
         psum_t = ctx.enter_context(tc.psum_pool(name="psum_t", bufs=4))
         psum_z = ctx.enter_context(tc.psum_pool(name="psum_z", bufs=2))
-        psum_o = ctx.enter_context(tc.psum_pool(name="psum_o", bufs=2))
+        psum_h = ctx.enter_context(tc.psum_pool(name="psum_h", bufs=2))
         ctx.enter_context(tc.manual_schedule())
 
         h1_sb = keep.tile([P, CHUNKS * HID], BF16)
@@ -95,7 +92,8 @@ def tile_gin_pb_kernel(tc, A, h1, eps1, W1_1, b1_1, out):
             out=rows[0:1, HID : HID + 1], in_=eps1.rearrange("(r o) -> r o", r=1)
         )
         nc.sync.dma_start(out=rows[0:1, 0:HID], in_=b1_1.rearrange("(r o) -> r o", r=1))
-        load_a_pair(1)
+        load_a(2)
+        load_a(3)
         nc.sync.dma_start(
             out=w_sb[:].rearrange("p (v r) -> p v r", v=2),
             in_=W1_1.rearrange("(v p e) o -> p v (e o)", v=2, e=2),
@@ -178,7 +176,8 @@ def tile_gin_pb_kernel(tc, A, h1, eps1, W1_1, b1_1, out):
         o_banks = {}
 
         def aggregate(c):
-            z_banks[c] = psum_z.tile([P, PACK, P], F32, name="z_bank", tag="z_bank")
+            pool, tag = (psum_h, "h_bank") if c in (HALF, HALF + 1) else (psum_z, "z_bank")
+            z_banks[c] = pool.tile([P, PACK, P], F32, name="z_bank", tag=tag)
             for t in range(PACK):
                 for g in range(NODE_PASSES):
                     feats = slice(g * HID + t * P, g * HID + (t + 1) * P)
@@ -212,7 +211,7 @@ def tile_gin_pb_kernel(tc, A, h1, eps1, W1_1, b1_1, out):
             )
 
         def linear(c):
-            o_banks[c] = psum_o.tile([P, HID], F32, name="o_bank", tag="o_bank")
+            o_banks[c] = psum_t.tile([P, HID], F32, name="o_bank", tag="t")
             nc.tensor.matmul_mx(
                 out=o_banks[c][:],
                 lhsT=z_codes[:, c * P : (c + 1) * P].bitcast(FP8X4),
@@ -250,8 +249,8 @@ def tile_gin_pb_kernel(tc, A, h1, eps1, W1_1, b1_1, out):
         transpose_h1(0, psum_t, "t")
         transpose_h1(1, psum_z, "z_bank")
         keep_clock_up(1)
-        transpose_h1(2, psum_o, "o_bank")
-        transpose_h1(3, psum_o, "o_bank")
+        transpose_h1(2, psum_h, "h_bank")
+        transpose_h1(3, psum_h, "h_bank")
         keep_clock_up(1)
         copy_h1_transposed(0)
         copy_h1_transposed(1)
@@ -261,59 +260,64 @@ def tile_gin_pb_kernel(tc, A, h1, eps1, W1_1, b1_1, out):
         nc.scalar.copy(out=h_slots[:, 1, 1], in_=h1_rows[:, 1, 1])
         quantise_h1(0)
         quantise_h1(1)
-        for c in range(PAIRS):
-            transpose_a(c)
-            if c < 2:
-                keep_clock_up(1)
-            if c == 1:
-                eps_bank = psum_t.tile([P, 16], F32, name="eps_bank", tag="t")
-                nc.tensor.matmul(
-                    out=eps_bank[:],
-                    lhsT=ones[:],
-                    rhs=rows[:, HID : HID + 16],
-                    start=True,
-                    stop=True,
-                )
-        for c in range(3):
-            quantise_a(c)
-            if c == 1:
-                nc.vector.tensor_scalar(
-                    out=self_w[:], in0=eps_bank[:, 0:1], scalar1=1.0, scalar2=None, op0=ALU.add
-                )
+        transpose_a(0)
+        transpose_a(1)
+        eps_bank = psum_t.tile([P, 16], F32, name="eps_bank", tag="t")
+        nc.tensor.matmul(
+            out=eps_bank[:], lhsT=ones[:], rhs=rows[:, HID : HID + 16], start=True, stop=True
+        )
+        transpose_a(2)
+        copy_h1_transposed(2)
+        transpose_a(3)
+        quantise_a(0)
+        quantise_a(1)
+        nc.vector.tensor_scalar(
+            out=self_w[:], in0=eps_bank[:, 0:1], scalar1=1.0, scalar2=None, op0=ALU.add
+        )
+        quantise_a(2)
+        aggregate(0)
+        aggregate(1)
+        regroup_w(0)
+        regroup_w(1)
+        transpose_a(4)
+        regroup_w(2)
+        transpose_a(5)
+        regroup_w(3)
 
-        for step in range(CHUNKS + BEHIND_BIAS):
-            if step % 2 == 0:
-                if step == BEHIND_BIAS:
-                    nc.vector.quantize_mx(
-                        out=w_codes[:].bitcast(FP8X4), scales=w_scales[:], in_=w_grouped[:]
-                    )
-                for c in (step, step + 1):
-                    if c < CHUNKS:
-                        aggregate(c)
-                    if 0 <= c - BEHIND_BIAS < CHUNKS:
-                        linear(c - BEHIND_BIAS)
-                if step + AHEAD_TRANSPOSE < CHUNKS:
-                    regroup_w(step)
-                    regroup_w(step + 1)
-                if step == 2:
-                    copy_h1_transposed(2)
-                    b_bank = psum_t.tile([P, HID], F32, name="b_bank", tag="t")
-                    nc.tensor.matmul(
-                        out=b_bank[:], lhsT=ones[:], rhs=rows[:, 0:HID], start=True, stop=True
-                    )
-                    nc.scalar.copy(out=b_all[:], in_=b_bank[:])
-                if step + AHEAD_TRANSPOSE < CHUNKS:
-                    transpose_a(step + AHEAD_TRANSPOSE)
-                    transpose_a(step + AHEAD_TRANSPOSE + 1)
-                if step == 2:
-                    copy_h1_transposed(3)
-            if step < CHUNKS:
-                add_self_term(step)
-            if step == 0:
+        for c in range(HALF):
+            if c > 0:
+                quantise_z(c - 1)
+            add_self_term(c)
+            if c == 0:
                 quantise_a(3)
-            elif 4 <= step + AHEAD_QUANTISE < CHUNKS:
-                quantise_a(step + AHEAD_QUANTISE)
-            if 0 <= step - BEHIND_QUANTISE_Z < CHUNKS:
-                quantise_z(step - BEHIND_QUANTISE_Z)
-            if step >= BEHIND_BIAS:
-                bias_relu_store(step - BEHIND_BIAS)
+            if c >= 2:
+                quantise_a(c + 2)
+            if c < 2:
+                aggregate(c + 2)
+        b_bank = psum_t.tile([P, HID], F32, name="b_bank", tag="t")
+        nc.tensor.matmul(
+            out=b_bank[:], lhsT=ones[:], rhs=rows[:, 0:HID], start=True, stop=True
+        )
+        transpose_a(6)
+        nc.scalar.copy(out=b_all[:], in_=b_bank[:])
+        copy_h1_transposed(3)
+        transpose_a(7)
+        nc.vector.quantize_mx(
+            out=w_codes[:].bitcast(FP8X4), scales=w_scales[:], in_=w_grouped[:]
+        )
+
+        for c in (HALF, HALF + 1):
+            aggregate(c)
+            linear(c - HALF)
+        for c in range(HALF, CHUNKS + HALF):
+            if c <= CHUNKS:
+                quantise_z(c - 1)
+            if c < CHUNKS:
+                add_self_term(c)
+            if c + 2 < CHUNKS:
+                quantise_a(c + 2)
+            bias_relu_store(c - HALF)
+            if c + 2 < CHUNKS:
+                aggregate(c + 2)
+            if c + 2 < CHUNKS + HALF:
+                linear(c + 2 - HALF)

@@ -22,6 +22,7 @@ PAIRS = CHUNKS // 2
 ROW_WORDS = NODES // 2
 HID_WORDS = HID // 2
 
+CLOCK_COLS = 320
 HALF = CHUNKS // 2
 
 FLOPS = 2 * NODES * NODES * HID + 2 * NODES * HID * HID
@@ -94,11 +95,12 @@ def tile_gin_pb_kernel(tc, A, h1, eps1, W1_1, b1_1, out):
         nc.sync.dma_start(out=rows[0:1, 0:HID], in_=b1_1.rearrange("(r o) -> r o", r=1))
         load_a(2)
         load_a(3)
+        load_a(4)
         nc.sync.dma_start(
             out=w_sb[:].rearrange("p (v r) -> p v r", v=2),
             in_=W1_1.rearrange("(v p e) o -> p v (e o)", v=2, e=2),
         )
-        load_a_pair(2)
+        load_a(5)
         load_a_pair(3)
 
         make_identity(nc, ident[:])
@@ -239,19 +241,21 @@ def tile_gin_pb_kernel(tc, A, h1, eps1, W1_1, b1_1, out):
 
         head_bank = psum_z.tile([P, HID], F32, name="head_bank", tag="z_bank")
 
-        def keep_clock_up(times):
-            for i in range(times):
-                nc.tensor.matmul(
-                    out=head_bank[:], lhsT=ones[:], rhs=zeros[:], start=True, stop=True
-                )
+        def keep_clock_up(cols):
+            nc.tensor.matmul(
+                out=head_bank[:, 0:cols], lhsT=ones[:], rhs=zeros[:, 0:cols], start=True, stop=True
+            )
 
-        keep_clock_up(4)
+        for i in range(4):
+            keep_clock_up(HID)
         transpose_h1(0, psum_t, "t")
+        keep_clock_up(CLOCK_COLS)
         transpose_h1(1, psum_z, "z_bank")
-        keep_clock_up(1)
+        keep_clock_up(CLOCK_COLS)
         transpose_h1(2, psum_h, "h_bank")
+        keep_clock_up(CLOCK_COLS)
         transpose_h1(3, psum_h, "h_bank")
-        keep_clock_up(1)
+        keep_clock_up(CLOCK_COLS)
         copy_h1_transposed(0)
         copy_h1_transposed(1)
         regroup_h1(0, 0)
@@ -261,12 +265,15 @@ def tile_gin_pb_kernel(tc, A, h1, eps1, W1_1, b1_1, out):
         quantise_h1(0)
         quantise_h1(1)
         transpose_a(0)
+        keep_clock_up(CLOCK_COLS)
         transpose_a(1)
+        keep_clock_up(CLOCK_COLS)
         eps_bank = psum_t.tile([P, 16], F32, name="eps_bank", tag="t")
         nc.tensor.matmul(
             out=eps_bank[:], lhsT=ones[:], rhs=rows[:, HID : HID + 16], start=True, stop=True
         )
         transpose_a(2)
+        keep_clock_up(CLOCK_COLS)
         copy_h1_transposed(2)
         transpose_a(3)
         quantise_a(0)
@@ -278,18 +285,18 @@ def tile_gin_pb_kernel(tc, A, h1, eps1, W1_1, b1_1, out):
         aggregate(0)
         aggregate(1)
         regroup_w(0)
-        regroup_w(1)
         transpose_a(4)
+        regroup_w(1)
         regroup_w(2)
         transpose_a(5)
         regroup_w(3)
 
         for c in range(HALF):
-            if c > 0:
-                quantise_z(c - 1)
             add_self_term(c)
             if c == 0:
                 quantise_a(3)
+            else:
+                quantise_z(c - 1)
             if c >= 2:
                 quantise_a(c + 2)
             if c < 2:
@@ -299,8 +306,8 @@ def tile_gin_pb_kernel(tc, A, h1, eps1, W1_1, b1_1, out):
             out=b_bank[:], lhsT=ones[:], rhs=rows[:, 0:HID], start=True, stop=True
         )
         transpose_a(6)
-        nc.scalar.copy(out=b_all[:], in_=b_bank[:])
         copy_h1_transposed(3)
+        nc.scalar.copy(out=b_all[:], in_=b_bank[:])
         transpose_a(7)
         nc.vector.quantize_mx(
             out=w_codes[:].bitcast(FP8X4), scales=w_scales[:], in_=w_grouped[:]
@@ -310,10 +317,10 @@ def tile_gin_pb_kernel(tc, A, h1, eps1, W1_1, b1_1, out):
             aggregate(c)
             linear(c - HALF)
         for c in range(HALF, CHUNKS + HALF):
-            if c <= CHUNKS:
-                quantise_z(c - 1)
             if c < CHUNKS:
                 add_self_term(c)
+            if c <= CHUNKS:
+                quantise_z(c - 1)
             if c + 2 < CHUNKS:
                 quantise_a(c + 2)
             bias_relu_store(c - HALF)

@@ -23,6 +23,7 @@ ROW_WORDS = NODES // 2
 HID_WORDS = HID // 2
 
 CLOCK_COLS = 320
+SIDE = (1, 2)
 HALF = CHUNKS // 2
 
 FLOPS = 2 * NODES * NODES * HID + 2 * NODES * HID * HID
@@ -63,6 +64,8 @@ def tile_gin_pb_kernel(tc, A, h1, eps1, W1_1, b1_1, out):
         zeros = keep.tile([P, HID], BF16)
         rows = keep.tile([P, HID + 16], BF16)
         b_all = keep.tile([P, HID], F32)
+        b_col = keep.tile([P, PACK], F32)
+        side_sb = keep.tile([P, PACK, len(SIDE) * P], F32)
         self_w = keep.tile([P, 1], F32)
         warm = keep.tile([P, 1], F32)
 
@@ -176,6 +179,7 @@ def tile_gin_pb_kernel(tc, A, h1, eps1, W1_1, b1_1, out):
 
         z_banks = {}
         o_banks = {}
+        side_banks = {}
 
         def aggregate(c):
             pool, tag = (psum_h, "h_bank") if c in (HALF, HALF + 1) else (psum_z, "z_bank")
@@ -224,6 +228,42 @@ def tile_gin_pb_kernel(tc, A, h1, eps1, W1_1, b1_1, out):
                 stop=True,
             )
 
+        def linear_transposed():
+            for half in range(2):
+                side_banks[half] = psum_t.tile([P, 2, len(SIDE) * P], F32, name="side", tag="t")
+                nodes = slice(SIDE[0] * P, (SIDE[-1] + 1) * P)
+                for i in range(2):
+                    outs = slice((2 * half + i) * P, (2 * half + i + 1) * P)
+                    nc.tensor.matmul_mx(
+                        out=side_banks[half][:, i, :],
+                        lhsT=w_codes[:, outs].bitcast(FP8X4),
+                        lhsT_scale=w_scales[:, outs],
+                        rhs=z_codes[:, nodes].bitcast(FP8X4),
+                        rhs_scale=z_scales[:, nodes],
+                        start=True,
+                        stop=True,
+                    )
+
+        def bias_relu_transposed():
+            for t in range(PACK):
+                nc.scalar.activation(
+                    out=side_sb[:, t, :],
+                    in_=side_banks[t // 2][:, t % 2, :],
+                    func=ACT.Relu,
+                    bias=b_col[:, t : t + 1],
+                )
+
+        def transpose_back_store(c):
+            bank = psum_h.tile([P, HID], F32, name="back_bank", tag="h_bank")
+            first = (c - SIDE[0]) * P
+            for t in range(PACK):
+                nc.tensor.transpose(
+                    bank[:, t * P : (t + 1) * P], side_sb[:, t, first : first + P], ident[:]
+                )
+            cols = slice(c * HID, (c + 1) * HID)
+            nc.scalar.copy(out=o_sb[:, cols], in_=bank[:])
+            nc.sync.dma_start(out=out_rows[:, c // 2, c % 2, :], in_=o_sb[:, cols])
+
         def bias_relu_store(c):
             width = HID // 2 if c == CHUNKS - 1 else HID
             for o in range(0, HID, width):
@@ -268,10 +308,22 @@ def tile_gin_pb_kernel(tc, A, h1, eps1, W1_1, b1_1, out):
         keep_clock_up(CLOCK_COLS)
         transpose_a(1)
         keep_clock_up(CLOCK_COLS)
-        eps_bank = psum_t.tile([P, 16], F32, name="eps_bank", tag="t")
+        head_row = psum_t.tile([P, PACK + 1, 16], F32, name="head_row", tag="t")
         nc.tensor.matmul(
-            out=eps_bank[:], lhsT=ones[:], rhs=rows[:, HID : HID + 16], start=True, stop=True
+            out=head_row[:, PACK, :],
+            lhsT=ones[:],
+            rhs=rows[:, HID : HID + 16],
+            start=True,
+            stop=True,
         )
+        for t in range(PACK):
+            nc.tensor.matmul(
+                out=head_row[:, t, :],
+                lhsT=rows[:, t * P : (t + 1) * P],
+                rhs=ones[:, 0:16],
+                start=True,
+                stop=True,
+            )
         transpose_a(2)
         keep_clock_up(CLOCK_COLS)
         copy_h1_transposed(2)
@@ -279,28 +331,25 @@ def tile_gin_pb_kernel(tc, A, h1, eps1, W1_1, b1_1, out):
         quantise_a(0)
         quantise_a(1)
         nc.vector.tensor_scalar(
-            out=self_w[:], in0=eps_bank[:, 0:1], scalar1=1.0, scalar2=None, op0=ALU.add
+            out=self_w[:], in0=head_row[:, PACK, 0:1], scalar1=1.0, scalar2=None, op0=ALU.add
         )
+        nc.vector.tensor_copy(out=b_col[:], in_=head_row[:, 0:PACK, 0])
         quantise_a(2)
         aggregate(0)
         aggregate(1)
         regroup_w(0)
-        transpose_a(4)
         regroup_w(1)
+        transpose_a(4)
+
+        add_self_term(0)
+        quantise_a(3)
+        aggregate(2)
         regroup_w(2)
         transpose_a(5)
         regroup_w(3)
-
-        for c in range(HALF):
-            add_self_term(c)
-            if c == 0:
-                quantise_a(3)
-            else:
-                quantise_z(c - 1)
-            if c >= 2:
-                quantise_a(c + 2)
-            if c < 2:
-                aggregate(c + 2)
+        add_self_term(1)
+        quantise_z(0)
+        aggregate(3)
         b_bank = psum_t.tile([P, HID], F32, name="b_bank", tag="t")
         nc.tensor.matmul(
             out=b_bank[:], lhsT=ones[:], rhs=rows[:, 0:HID], start=True, stop=True
@@ -309,22 +358,33 @@ def tile_gin_pb_kernel(tc, A, h1, eps1, W1_1, b1_1, out):
         copy_h1_transposed(3)
         nc.scalar.copy(out=b_all[:], in_=b_bank[:])
         transpose_a(7)
+        for c in (2, 3):
+            add_self_term(c)
+            quantise_a(c + 2)
+            quantise_z(c - 1)
         nc.vector.quantize_mx(
             out=w_codes[:].bitcast(FP8X4), scales=w_scales[:], in_=w_grouped[:]
         )
+        aggregate(4)
+        linear(0)
+        aggregate(5)
+        linear_transposed()
+        bias_relu_transposed()
 
-        for c in (HALF, HALF + 1):
-            aggregate(c)
-            linear(c - HALF)
         for c in range(HALF, CHUNKS + HALF):
             if c < CHUNKS:
                 add_self_term(c)
-            if c <= CHUNKS:
-                quantise_z(c - 1)
             if c + 2 < CHUNKS:
                 quantise_a(c + 2)
-            bias_relu_store(c - HALF)
+            if c <= CHUNKS:
+                quantise_z(c - 1)
+            if c - HALF not in SIDE:
+                bias_relu_store(c - HALF)
             if c + 2 < CHUNKS:
                 aggregate(c + 2)
-            if c + 2 < CHUNKS + HALF:
-                linear(c + 2 - HALF)
+            if c == 5:
+                transpose_back_store(1)
+                linear(3)
+                transpose_back_store(2)
+            if 5 < c < CHUNKS + 2:
+                linear(c - 2)

from contextlib import ExitStack

import concourse.mybir as mybir
from concourse.masks import make_identity

F32 = mybir.dt.float32
BF16 = mybir.dt.bfloat16
U32 = mybir.dt.uint32
U8 = mybir.dt.uint8
FP8X4 = mybir.dt.float8_e4m3fn_x4
ALU = mybir.AluOpType
ACT = mybir.ActivationFunctionType

P = 128
PACK = 4
K_PASS = P * PACK
NODES = 1024
HID = 512
NODE_PASSES = NODES // K_PASS
CHUNKS = NODES // P
PAIRS = CHUNKS // 2
ROW_WORDS = NODES // 2
HID_WORDS = HID // 2

CLOCK_COLS = 320
SIDE = (1, 2)
HALF = CHUNKS // 2

FLOPS = 2 * NODES * NODES * HID + 2 * NODES * HID * HID


def tile_gin_pb_kernel(tc, A, h1, eps1, W1_1, b1_1, out):
    nc = tc.nc
    with ExitStack() as ctx:
        keep = ctx.enter_context(tc.tile_pool(name="keep", bufs=1))
        psum_t = ctx.enter_context(tc.psum_pool(name="psum_t", bufs=4))
        psum_z = ctx.enter_context(tc.psum_pool(name="psum_z", bufs=2))
        psum_h = ctx.enter_context(tc.psum_pool(name="psum_h", bufs=2))
        ctx.enter_context(tc.manual_schedule())

        h1_sb = keep.tile([P, CHUNKS * HID], BF16)
        a_sb = keep.tile([P, CHUNKS * NODES], BF16)
        w_sb = keep.tile([P, PACK * HID], BF16)

        h_grouped = keep.tile([P, NODE_PASSES * HID * PACK], BF16, align_bytes=64)
        h_codes = keep.tile([P, NODE_PASSES * HID], U32, align_bytes=64)
        h_scales = keep.tile([P, NODE_PASSES * HID], U8, align_bytes=64)
        w_grouped = keep.tile([P, HID * PACK], BF16, align_bytes=64)
        w_codes = keep.tile([P, HID], U32, align_bytes=64)
        w_scales = keep.tile([P, HID], U8, align_bytes=64)
        a_grouped = keep.tile([P, CHUNKS * NODE_PASSES * P * PACK], BF16, align_bytes=64)
        a_codes = keep.tile([P, CHUNKS * NODE_PASSES * P], U32, align_bytes=64)
        a_scales = keep.tile([P, CHUNKS * NODE_PASSES * P], U8, align_bytes=64)
        z_grouped = keep.tile([P, CHUNKS * P * PACK], BF16, align_bytes=64)
        z_codes = keep.tile([P, CHUNKS * P], U32, align_bytes=64)
        z_scales = keep.tile([P, CHUNKS * P], U8, align_bytes=64)

        hT_sb = keep.tile([P, CHUNKS * P * PACK], BF16)
        o_sum = keep.tile([P, CHUNKS * HID], F32)
        o_sb = keep.tile([P, CHUNKS * HID], F32)

        ident = keep.tile([P, P], F32)
        ones = keep.tile([P, P], BF16)
        zeros = keep.tile([P, HID], BF16)
        rows = keep.tile([P, HID + 16], BF16)
        b_all = keep.tile([P, HID], F32)
        b_col = keep.tile([P, PACK], F32)
        side_sb = keep.tile([P, PACK, len(SIDE) * P], F32)
        self_w = keep.tile([P, 1], F32)
        warm = keep.tile([P, 1], F32)

        a_rows = A.rearrange("(h p e) k -> p h e k", h=PAIRS, e=2)

        def load_a(c):
            nc.sync.dma_start(
                out=a_sb[:, c * NODES : (c + 1) * NODES], in_=a_rows[:, c // 2, c % 2, :]
            )

        def load_a_pair(h):
            nc.sync.dma_start(
                out=a_sb[:, 2 * h * NODES : 2 * (h + 1) * NODES],
                in_=A[h * 2 * P : (h + 1) * 2 * P, :].rearrange("(p e) k -> p (e k)", e=2),
            )

        nc.vector.memset(zeros[:].bitcast(U32), 0)
        nc.vector.memset(ones[:], 1.0)
        nc.vector.memset(rows[:].bitcast(U32), 0)
        for h in range(PAIRS):
            nc.sync.dma_start(
                out=h1_sb[:, h * 2 * HID : (h + 1) * 2 * HID],
                in_=h1[h * 2 * P : (h + 1) * 2 * P, :].rearrange("(p e) f -> p (e f)", e=2),
            )
        load_a(0)
        load_a(1)
        nc.sync.dma_start(
            out=rows[0:1, HID : HID + 1], in_=eps1.rearrange("(r o) -> r o", r=1)
        )
        nc.sync.dma_start(out=rows[0:1, 0:HID], in_=b1_1.rearrange("(r o) -> r o", r=1))
        load_a(2)
        load_a(3)
        load_a(4)
        nc.sync.dma_start(
            out=w_sb[:].rearrange("p (v r) -> p v r", v=2),
            in_=W1_1.rearrange("(v p e) o -> p v (e o)", v=2, e=2),
        )
        load_a(5)
        load_a_pair(3)

        make_identity(nc, ident[:])
        nc.scalar.activation(out=warm[:], in_=ones[:, 0:1], func=ACT.Relu)

        h1_rows = h1_sb[:].rearrange(
            "p (g t v q e) -> p g v q t e", g=NODE_PASSES, t=PACK, v=2, e=2
        )
        h_slots = h_grouped[:].rearrange(
            "p (g v e q t) -> p g v q t e", g=NODE_PASSES, v=2, e=2, t=PACK
        )
        h1_words = h1_sb[:].bitcast(F32)
        hT_words = hT_sb[:].bitcast(F32).rearrange("p (c n v) -> p c n v", c=CHUNKS, v=2)
        a_words = a_sb[:].bitcast(F32)
        a_slots = a_grouped[:].bitcast(F32).rearrange(
            "p (c g n u) -> p c g n u", c=CHUNKS, g=NODE_PASSES, u=2
        )
        w_rows = w_sb[:].rearrange("p (t o) -> p t o", t=PACK)
        w_slots = w_grouped[:].rearrange("p (o t) -> p o t", t=PACK)
        out_rows = out.rearrange("(h p e) o -> p h e o", h=PAIRS, e=2)

        h_banks = {}

        def transpose_h1(h, pool, tag):
            h_banks[h] = pool.tile([P, 2, 2, P], F32, name="hT_bank", tag=tag)
            for i in range(2):
                for v in range(2):
                    first = (2 * h + i) * HID_WORDS + v * P
                    nc.tensor.transpose(
                        h_banks[h][:, i, v, :], h1_words[:, first : first + P], ident[:]
                    )

        def copy_h1_transposed(h):
            nc.scalar.copy(
                out=hT_words[:, 2 * h : 2 * h + 2],
                in_=h_banks[h][:].rearrange("p i v n -> p i n v"),
            )

        def regroup_h1(g, v):
            nc.vector.tensor_copy(out=h_slots[:, g, v], in_=h1_rows[:, g, v])

        def quantise_h1(g):
            nc.vector.quantize_mx(
                out=h_codes[:, g * HID : (g + 1) * HID].bitcast(FP8X4),
                scales=h_scales[:, g * HID : (g + 1) * HID],
                in_=h_grouped[:, g * HID * PACK : (g + 1) * HID * PACK],
            )

        def regroup_w(quarter):
            outs = slice(quarter * P, (quarter + 1) * P)
            nc.scalar.copy(
                out=w_slots[:, outs].rearrange("p (c i) t -> p c t i", i=4),
                in_=w_rows[:, :, outs].rearrange("p t (c i) -> p c t i", i=4),
            )

        def transpose_a(c):
            a_bank = psum_t.tile([P, NODE_PASSES, 2, P], F32, tag="t")
            for g in range(NODE_PASSES):
                for u in range(2):
                    first = c * ROW_WORDS + (2 * g + u) * P
                    nc.tensor.transpose(
                        a_bank[:, g, u, :], a_words[:, first : first + P], ident[:]
                    )
            nc.scalar.copy(out=a_slots[:, c], in_=a_bank[:].rearrange("p g u n -> p g n u"))

        def quantise_a(c):
            width = NODE_PASSES * P
            nc.vector.quantize_mx(
                out=a_codes[:, c * width : (c + 1) * width].bitcast(FP8X4),
                scales=a_scales[:, c * width : (c + 1) * width],
                in_=a_grouped[:, c * width * PACK : (c + 1) * width * PACK],
            )

        z_banks = {}
        o_banks = {}
        side_banks = {}

        def aggregate(c):
            pool, tag = (psum_h, "h_bank") if c in (HALF, HALF + 1) else (psum_z, "z_bank")
            z_banks[c] = pool.tile([P, PACK, P], F32, name="z_bank", tag=tag)
            for t in range(PACK):
                for g in range(NODE_PASSES):
                    feats = slice(g * HID + t * P, g * HID + (t + 1) * P)
                    nodes = slice((c * NODE_PASSES + g) * P, (c * NODE_PASSES + g + 1) * P)
                    nc.tensor.matmul_mx(
                        out=z_banks[c][:, t, :],
                        lhsT=h_codes[:, feats].bitcast(FP8X4),
                        lhsT_scale=h_scales[:, feats],
                        rhs=a_codes[:, nodes].bitcast(FP8X4),
                        rhs_scale=a_scales[:, nodes],
                        start=(g == 0),
                        stop=(g == NODE_PASSES - 1),
                    )

        def add_self_term(c):
            cols = slice(c * P * PACK, (c + 1) * P * PACK)
            nc.vector.scalar_tensor_tensor(
                out=z_grouped[:, cols].rearrange("p (n t) -> p n t", t=PACK),
                in0=hT_sb[:, cols].rearrange("p (n t) -> p n t", t=PACK),
                scalar=self_w[:, 0:1],
                in1=z_banks[c][:].rearrange("p t n -> p n t"),
                op0=ALU.mult,
                op1=ALU.add,
            )

        def quantise_z(c):
            nc.vector.quantize_mx(
                out=z_codes[:, c * P : (c + 1) * P].bitcast(FP8X4),
                scales=z_scales[:, c * P : (c + 1) * P],
                in_=z_grouped[:, c * P * PACK : (c + 1) * P * PACK],
            )

        def linear(c):
            o_banks[c] = psum_t.tile([P, HID], F32, name="o_bank", tag="t")
            nc.tensor.matmul_mx(
                out=o_banks[c][:],
                lhsT=z_codes[:, c * P : (c + 1) * P].bitcast(FP8X4),
                lhsT_scale=z_scales[:, c * P : (c + 1) * P],
                rhs=w_codes[:].bitcast(FP8X4),
                rhs_scale=w_scales[:],
                start=True,
                stop=True,
            )

        def linear_transposed():
            for half in range(2):
                side_banks[half] = psum_t.tile([P, 2, len(SIDE) * P], F32, name="side", tag="t")
                nodes = slice(SIDE[0] * P, (SIDE[-1] + 1) * P)
                for i in range(2):
                    outs = slice((2 * half + i) * P, (2 * half + i + 1) * P)
                    nc.tensor.matmul_mx(
                        out=side_banks[half][:, i, :],
                        lhsT=w_codes[:, outs].bitcast(FP8X4),
                        lhsT_scale=w_scales[:, outs],
                        rhs=z_codes[:, nodes].bitcast(FP8X4),
                        rhs_scale=z_scales[:, nodes],
                        start=True,
                        stop=True,
                    )

        def bias_relu_transposed():
            for t in range(PACK):
                nc.scalar.activation(
                    out=side_sb[:, t, :],
                    in_=side_banks[t // 2][:, t % 2, :],
                    func=ACT.Relu,
                    bias=b_col[:, t : t + 1],
                )

        def transpose_back_store(c):
            bank = psum_h.tile([P, HID], F32, name="back_bank", tag="h_bank")
            first = (c - SIDE[0]) * P
            for t in range(PACK):
                nc.tensor.transpose(
                    bank[:, t * P : (t + 1) * P], side_sb[:, t, first : first + P], ident[:]
                )
            cols = slice(c * HID, (c + 1) * HID)
            nc.scalar.copy(out=o_sb[:, cols], in_=bank[:])
            nc.sync.dma_start(out=out_rows[:, c // 2, c % 2, :], in_=o_sb[:, cols])

        def bias_relu_store(c):
            width = HID // 2 if c == CHUNKS - 1 else HID
            for o in range(0, HID, width):
                cols = slice(c * HID + o, c * HID + o + width)
                nc.vector.tensor_tensor(
                    out=o_sum[:, cols],
                    in0=o_banks[c][:, o : o + width],
                    in1=b_all[:, o : o + width],
                    op=ALU.add,
                )
                nc.scalar.activation(out=o_sb[:, cols], in_=o_sum[:, cols], func=ACT.Relu)
                nc.sync.dma_start(
                    out=out_rows[:, c // 2, c % 2, o : o + width], in_=o_sb[:, cols]
                )

        head_bank = psum_z.tile([P, HID], F32, name="head_bank", tag="z_bank")

        def keep_clock_up(cols):
            nc.tensor.matmul(
                out=head_bank[:, 0:cols], lhsT=ones[:], rhs=zeros[:, 0:cols], start=True, stop=True
            )

        for i in range(4):
            keep_clock_up(HID)
        transpose_h1(0, psum_t, "t")
        keep_clock_up(CLOCK_COLS)
        transpose_h1(1, psum_z, "z_bank")
        keep_clock_up(CLOCK_COLS)
        transpose_h1(2, psum_h, "h_bank")
        keep_clock_up(CLOCK_COLS)
        transpose_h1(3, psum_h, "h_bank")
        keep_clock_up(CLOCK_COLS)
        copy_h1_transposed(0)
        copy_h1_transposed(1)
        regroup_h1(0, 0)
        regroup_h1(0, 1)
        regroup_h1(1, 0)
        nc.scalar.copy(out=h_slots[:, 1, 1], in_=h1_rows[:, 1, 1])
        quantise_h1(0)
        quantise_h1(1)
        transpose_a(0)
        keep_clock_up(CLOCK_COLS)
        transpose_a(1)
        keep_clock_up(CLOCK_COLS)
        head_row = psum_t.tile([P, PACK + 1, 16], F32, name="head_row", tag="t")
        nc.tensor.matmul(
            out=head_row[:, PACK, :],
            lhsT=ones[:],
            rhs=rows[:, HID : HID + 16],
            start=True,
            stop=True,
        )
        for t in range(PACK):
            nc.tensor.matmul(
                out=head_row[:, t, :],
                lhsT=rows[:, t * P : (t + 1) * P],
                rhs=ones[:, 0:16],
                start=True,
                stop=True,
            )
        transpose_a(2)
        keep_clock_up(CLOCK_COLS)
        copy_h1_transposed(2)
        transpose_a(3)
        quantise_a(0)
        quantise_a(1)
        nc.vector.tensor_scalar(
            out=self_w[:], in0=head_row[:, PACK, 0:1], scalar1=1.0, scalar2=None, op0=ALU.add
        )
        nc.vector.tensor_copy(out=b_col[:], in_=head_row[:, 0:PACK, 0])
        quantise_a(2)
        aggregate(0)
        aggregate(1)
        regroup_w(0)
        regroup_w(1)
        transpose_a(4)

        add_self_term(0)
        quantise_a(3)
        aggregate(2)
        regroup_w(2)
        transpose_a(5)
        regroup_w(3)
        add_self_term(1)
        quantise_z(0)
        aggregate(3)
        b_bank = psum_t.tile([P, HID], F32, name="b_bank", tag="t")
        nc.tensor.matmul(
            out=b_bank[:], lhsT=ones[:], rhs=rows[:, 0:HID], start=True, stop=True
        )
        transpose_a(6)
        copy_h1_transposed(3)
        nc.scalar.copy(out=b_all[:], in_=b_bank[:])
        transpose_a(7)
        for c in (2, 3):
            add_self_term(c)
            quantise_a(c + 2)
            quantise_z(c - 1)
        nc.vector.quantize_mx(
            out=w_codes[:].bitcast(FP8X4), scales=w_scales[:], in_=w_grouped[:]
        )
        aggregate(4)
        linear(0)
        aggregate(5)
        linear_transposed()
        bias_relu_transposed()

        for c in range(HALF, CHUNKS + HALF):
            if c < CHUNKS:
                add_self_term(c)
            if c + 2 < CHUNKS:
                quantise_a(c + 2)
            if c <= CHUNKS:
                quantise_z(c - 1)
            if c - HALF not in SIDE:
                bias_relu_store(c - HALF)
            if c + 2 < CHUNKS:
                aggregate(c + 2)
            if c == 5:
                transpose_back_store(1)
                linear(3)
                transpose_back_store(2)
            if 5 < c < CHUNKS + 2:
                linear(c - 2)
